import numpy as np
import ml_dtypes


def mxq(x, axis, fmt="e4m3"):
    dtype, down = {"e4m3": (ml_dtypes.float8_e4m3fn, 7), "e5m2": (ml_dtypes.float8_e5m2, 14)}[fmt]
    v = np.moveaxis(np.asarray(x, np.float32).astype(ml_dtypes.bfloat16).astype(np.float64), axis, -1)
    blocks = v.reshape(v.shape[:-1] + (-1, 32))
    amax = np.abs(blocks).max(-1, keepdims=True)
    byte = np.maximum(np.where(amax > 0, np.frexp(amax)[1] - 1 + 127, 0) - down, 1)
    scale = np.exp2(byte - 127.0)
    codes = (blocks / scale).astype(np.float32).astype(dtype).astype(np.float64)
    return np.moveaxis((codes * scale).reshape(v.shape), -1, axis)


WIDE = False


def mx_kscale(k):
    if not WIDE:
        return np.ones(k)
    levels = np.array([10, -10, 5, -5, 0])
    a = np.random.permutation(np.resize(levels, k // 512 * 4)).reshape(k // 512, 4)
    idx = np.arange(k)
    return np.exp2(a[idx // 512, idx % 128 // 32])


BF16 = ml_dtypes.bfloat16


def bf(x):
    return np.asarray(x, np.float32).astype(BF16)


def f64(x):
    return np.asarray(x).astype(np.float64)


B, N, D, GROUP, E1, S1, E2, HID = 4, 4096, 512, 512, 8, 16, 4, 1024
G = N // GROUP
NS = S1 // E2
M = S1 // NS
P2 = E2 * M
R = B * G * M
EPS = 1e-6
LG = 2.0


def l2norm(t):
    return t / np.sqrt(np.sum(t * t, axis=-1, keepdims=True) + EPS)


def setup_inputs():
    s = mx_kscale(D)
    c = np.sqrt(np.mean(1.0 / s**2))
    y = LG / np.sqrt(D) * np.random.standard_normal((B, G, E1, S1, D)) * s * c
    return {"yn": bf(y),
            "means": bf(y.reshape(B, G, E1, M, NS, D).mean(axis=4)),
            "w_slot2": bf(np.random.standard_normal((E1, D, E2 * D)) / s[:, None] / np.tile(s, E2))}


def reference(yn, means, w_slot2):
    mk = f64(means).transpose(2, 0, 1, 3, 4).reshape(E1, R, D)
    se = mxq(mk, 2, "e4m3") @ mxq(f64(w_slot2), 1, "e4m3")
    se = se.reshape(E1, B, G, M, E2, D).transpose(1, 2, 0, 4, 3, 5)
    se2 = (l2norm(se) * np.sqrt(D)).reshape(B, G, E1, P2, D)
    logits = mxq(f64(yn), 4, "e4m3") @ mxq(se2, 4, "e4m3").swapaxes(3, 4)
    a = np.exp(logits - logits.max(axis=3, keepdims=True))
    disp2 = a / a.sum(axis=3, keepdims=True)
    c = np.exp(logits - logits.max(axis=4, keepdims=True))
    comb2 = c / c.sum(axis=4, keepdims=True)
    return disp2, comb2

@@ -1,0 +1,350 @@
+from contextlib import ExitStack
+
+import concourse.mybir as mybir
+from concourse.masks import make_identity
+
+FP32 = mybir.dt.float32
+BF16 = mybir.dt.bfloat16
+U32 = mybir.dt.uint32
+U8 = mybir.dt.uint8
+FP8X4 = mybir.dt.float8_e4m3fn_x4
+ALU = mybir.AluOpType
+ACT = mybir.ActivationFunctionType
+AXIS = mybir.AxisListType
+
+P = 128
+PACK = 4
+GROUPS = 32
+OUTER = 8
+TOKENS = 16
+INNER = 4
+SEGMENTS = 4
+SLOTS = INNER * SEGMENTS
+D = 512
+ROWS = GROUPS * SEGMENTS
+OCTET = P // TOKENS
+OCTETS = GROUPS // OCTET
+EPS = 1e-6
+
+CHUNKS = OUTER * INNER
+MEAN_TILES = GROUPS * OUTER * SEGMENTS // P
+YN_BANKS = GROUPS // 2
+
+VECTOR_WORDS = 60
+
+PREFETCH = 6
+QUANTISE_LAG = 1
+SQUARE_LAG = 2
+SPREAD_LAG = 3
+NORMALISE_LAG = 4
+SLOTS_LAG = 8
+LOGITS_LAG = 14
+YN_FIRST_STEP = 4
+YN_QUANTISE_STEP = YN_FIRST_STEP + YN_BANKS // 2 + 1
+LAST_STEP = INNER * (OUTER - 1) + LOGITS_LAG + 4
+
+FLOPS = 2 * OUTER * ROWS * D * INNER * D + 2 * GROUPS * OUTER * TOKENS * SLOTS * D
+
+
+def tile_hierarchicalsoftmoe2dblock_pb_kernel(tc, yn, means, w_slot2, out_0, out_1):
+    nc = tc.nc
+    with ExitStack() as ctx:
+        ctx.enter_context(tc.manual_schedule())
+        keep = ctx.enter_context(tc.tile_pool(name="keep", bufs=1))
+        w_pool = ctx.enter_context(tc.tile_pool(name="w_pool", bufs=PREFETCH + 2))
+        grouped_pool = ctx.enter_context(tc.tile_pool(name="grouped_pool", bufs=3))
+        codes_pool = ctx.enter_context(tc.tile_pool(name="codes_pool", bufs=SPREAD_LAG + 2))
+        work = ctx.enter_context(tc.tile_pool(name="work", bufs=2))
+        small = ctx.enter_context(tc.tile_pool(name="small", bufs=4))
+        psum = ctx.enter_context(tc.psum_pool(name="psum", bufs=2))
+
+        ident = keep.tile([P, P], FP32)
+        make_identity(nc, ident[:])
+        parity = keep.tile([P, 2], FP32)
+        nc.vector.tensor_reduce(
+            out=parity[:],
+            in_=ident[:].rearrange("p (q h c) -> p h q c", h=2, c=TOKENS),
+            axis=AXIS.XY,
+            op=ALU.add,
+        )
+        minus_half = keep.tile([P, 1], FP32)
+        nc.vector.memset(minus_half[:], -0.5)
+
+        mean_raw = keep.tile([P, MEAN_TILES, D], BF16)
+        mean_grouped = keep.tile([P, OUTER, ROWS, PACK], BF16, align_bytes=64)
+        mean_codes = keep.tile([P, OUTER, ROWS], U32, align_bytes=64)
+        mean_scales = keep.tile([P, OUTER, ROWS], U8, align_bytes=64)
+        yn_raw = keep.tile([P, GROUPS, D], BF16)
+        yn_grouped = keep.tile([P, OUTER, GROUPS, TOKENS, PACK], BF16, align_bytes=64)
+        yn_codes = keep.tile([P, OUTER, GROUPS * TOKENS], U32, align_bytes=64)
+        yn_scales = keep.tile([P, OUTER, GROUPS * TOKENS], U8, align_bytes=64)
+        se2_codes = keep.tile([P, OUTER, GROUPS * SLOTS], U32, align_bytes=64)
+        se2_scales = keep.tile([P, OUTER, GROUPS * SLOTS], U8, align_bytes=64)
+        logits_t = keep.tile([P, OCTETS, OUTER, TOKENS], FP32)
+        disp_t = keep.tile([P, OCTETS, OUTER, TOKENS], FP32)
+
+        w_raw, grouped, w_codes, w_scales = {}, {}, {}, {}
+        se_rows, norm_factor, spread_bank, spread, se_cols, se2_grouped = {}, {}, {}, {}, {}, {}
+        yn_bank, all_pairs, two_groups, powers = {}, {}, {}, {}
+
+        def transpose_two(words, first):
+            bank = psum.tile([P, 2, 2, P], FP32, tag="bank")
+            for a in range(2):
+                for u in range(2):
+                    nc.tensor.transpose(bank[:, a, u, :], words[:, first + a, u, :], ident[:])
+            return bank
+
+        mean_rows = means.flatten_outer_dims().rearrange("(a p) d -> p a d", p=P)
+        for half in (slice(0, MEAN_TILES // 2), slice(MEAN_TILES // 2, MEAN_TILES)):
+            nc.sync.dma_start(out=mean_raw[:, half, :], in_=mean_rows[:, half, :])
+        mean_words = mean_raw[:].bitcast(FP32).rearrange("p a (w u) -> p a u w", u=2)
+        mean_slots = mean_grouped[:].bitcast(FP32).rearrange(
+            "p k (a b m) u -> p a b k m u", a=MEAN_TILES, m=SEGMENTS
+        )
+
+        def quantise_means():
+            nc.vector.quantize_mx(
+                out=mean_codes[:].rearrange("p k r -> p (k r)").bitcast(FP8X4),
+                scales=mean_scales[:].rearrange("p k r -> p (k r)"),
+                in_=mean_grouped[:].rearrange("p k r t -> p (k r t)"),
+            )
+
+        yn_rows = yn.flatten_outer_dims().rearrange("(g p) d -> p g d", p=P)
+        yn_words = yn_raw[:].bitcast(FP32).rearrange("p g (w u) -> p g u w", u=2)
+        yn_slots = yn_grouped[:].bitcast(FP32).rearrange("p k g s u -> p g k s u")
+
+        def load_yn(i):
+            some = slice(i * OCTET, (i + 1) * OCTET)
+            nc.sync.dma_start(out=yn_raw[:, some, :], in_=yn_rows[:, some, :])
+
+        def transpose_yn(b):
+            yn_bank[b] = transpose_two(yn_words, 2 * b)
+
+        def copy_yn(b):
+            copy = nc.scalar.copy if b % 2 == 0 else nc.vector.tensor_copy
+            copy(
+                out=yn_slots[:, 2 * b : 2 * b + 2],
+                in_=yn_bank[b][:].rearrange("p g u (k s) -> p g k s u", k=OUTER),
+            )
+
+        def quantise_yn(pair):
+            two = slice(2 * pair, 2 * pair + 2)
+            nc.vector.quantize_mx(
+                out=yn_codes[:, two, :].rearrange("p k c -> p (k c)").bitcast(FP8X4),
+                scales=yn_scales[:, two, :].rearrange("p k c -> p (k c)"),
+                in_=yn_grouped[:, two].rearrange("p k g s t -> p (k g s t)"),
+            )
+
+        def load_chunk(c):
+            k, e = divmod(c, INNER)
+            w_raw[c] = w_pool.tile([P, PACK, D], BF16, name="w_raw")
+            rows = w_slot2[k].rearrange("(p j) n -> p j n", j=PACK)
+            nc.sync.dma_start(out=w_raw[c][:], in_=rows[:, :, e * D : (e + 1) * D])
+
+        def regroup(c):
+            grouped[c] = grouped_pool.tile([P, PACK, P, PACK], BF16, name="grouped", align_bytes=64)
+            to_words = grouped[c][:].rearrange("p t w j -> p w j t")
+            from_rows = w_raw[c][:].rearrange("p j (w t) -> p w j t", t=PACK)
+            nc.vector.tensor_copy(out=to_words[:, :VECTOR_WORDS], in_=from_rows[:, :VECTOR_WORDS])
+            nc.scalar.copy(out=to_words[:, VECTOR_WORDS:], in_=from_rows[:, VECTOR_WORDS:])
+
+        def quantise_chunk(c):
+            w_codes[c] = codes_pool.tile([P, D], U32, name="w_codes", align_bytes=64)
+            w_scales[c] = codes_pool.tile([P, D], U8, name="w_scales", align_bytes=64)
+            nc.vector.quantize_mx(
+                out=w_codes[c][:].bitcast(FP8X4),
+                scales=w_scales[c][:],
+                in_=grouped[c][:].rearrange("p t w j -> p (t w j)"),
+            )
+            se_rows[c] = psum.tile([P, D], FP32, name="se_rows")
+            nc.tensor.matmul_mx(
+                out=se_rows[c][:],
+                lhsT=mean_codes[:, c // INNER, :].bitcast(FP8X4),
+                lhsT_scale=mean_scales[:, c // INNER, :],
+                rhs=w_codes[c][:].bitcast(FP8X4),
+                rhs_scale=w_scales[c][:],
+                start=True,
+                stop=True,
+            )
+
+        def find_norm_factor(c):
+            squares = work.tile([P, D], BF16)
+            sum_squares = small.tile([P, 1], FP32)
+            nc.scalar.activation(out=squares[:], in_=se_rows[c][:], func=ACT.Square, accum_out=sum_squares[:])
+            mean_square = small.tile([P, 1], FP32)
+            nc.gpsimd.tensor_scalar(
+                out=mean_square[:], in0=sum_squares[:], scalar1=1.0 / D, scalar2=EPS / D, op0=ALU.mult, op1=ALU.add
+            )
+            norm_factor[c] = small.tile([P, 1], FP32, name="norm_factor")
+            nc.gpsimd.tensor_tensor(out=norm_factor[c][:], in0=mean_square[:], in1=minus_half[:], op=ALU.pow)
+
+        def spread_norm_factor(c):
+            spread_bank[c] = psum.tile([P, ROWS], FP32, name="spread_bank")
+            nc.tensor.transpose(spread_bank[c][:], norm_factor[c][:].to_broadcast([P, P]), ident[:])
+
+        def multiply_transposed(c):
+            spread[c] = work.tile([P, ROWS], FP32, name="spread", bufs=3)
+            nc.scalar.copy(out=spread[c][:], in_=spread_bank[c][:])
+            se_cols[c] = psum.tile([P, PACK, ROWS], FP32, name="se_cols")
+            for t in range(PACK):
+                block = slice(t * P, (t + 1) * P)
+                nc.tensor.matmul_mx(
+                    out=se_cols[c][:, t, :],
+                    lhsT=w_codes[c][:, block].bitcast(FP8X4),
+                    lhsT_scale=w_scales[c][:, block],
+                    rhs=mean_codes[:, c // INNER, :].bitcast(FP8X4),
+                    rhs_scale=mean_scales[:, c // INNER, :],
+                    start=True,
+                    stop=True,
+                )
+
+        def normalise(c):
+            k, e = divmod(c, INNER)
+            if e == 0:
+                se2_grouped[k] = work.tile(
+                    [P, GROUPS, INNER, SEGMENTS, PACK], BF16, name="se2_grouped", align_bytes=64
+                )
+            nc.vector.tensor_tensor(
+                out=se2_grouped[k][:, :, e, :, :],
+                in0=se_cols[c][:].rearrange("p t (g m) -> p g m t", m=SEGMENTS),
+                in1=spread[c][:]
+                .rearrange("p (g m) -> p g m", m=SEGMENTS)
+                .unsqueeze(3)
+                .to_broadcast([P, GROUPS, SEGMENTS, PACK]),
+                op=ALU.mult,
+            )
+
+        def quantise_slots(k):
+            nc.vector.quantize_mx(
+                out=se2_codes[:, k, :].bitcast(FP8X4),
+                scales=se2_scales[:, k, :],
+                in_=se2_grouped[k][:].rearrange("p g e m t -> p (g e m t)"),
+            )
+
+        def multiply_slots_and_tokens(k):
+            all_pairs[k] = psum.tile([P, OCTETS, P], FP32, tag="bank", name="all_pairs")
+            for i in range(OCTETS):
+                block = slice(i * P, (i + 1) * P)
+                nc.tensor.matmul_mx(
+                    out=all_pairs[k][:, i, :],
+                    lhsT=se2_codes[:, k, block].bitcast(FP8X4),
+                    lhsT_scale=se2_scales[:, k, block],
+                    rhs=yn_codes[:, k, block].bitcast(FP8X4),
+                    rhs_scale=yn_scales[:, k, block],
+                    start=True,
+                    stop=True,
+                )
+
+        def copy_quadrants(k):
+            two_groups[k] = work.tile([P, OCTETS, 2, TOKENS], FP32, name="two_groups")
+            for quadrant in range(4):
+                rows = slice(32 * quadrant, 32 * quadrant + 32)
+                nc.scalar.copy(
+                    out=two_groups[k][rows],
+                    in_=all_pairs[k][rows, :, 32 * quadrant : 32 * quadrant + 32].rearrange(
+                        "p i (h s) -> p i h s", h=2
+                    ),
+                )
+
+        def softmax_start(logits, sets):
+            shape = [P, sets, TOKENS]
+            top = small.tile([P, sets], FP32, name="top")
+            nc.vector.tensor_reduce(out=top[:], in_=logits, axis=AXIS.X, op=ALU.max)
+            shifted = work.tile(shape, FP32, name="shifted", bufs=3)
+            nc.vector.tensor_tensor(
+                out=shifted[:], in0=logits, in1=top[:].unsqueeze(2).to_broadcast(shape), op=ALU.subtract
+            )
+            return shifted
+
+        def softmax_end(shifted, result, sets):
+            total = small.tile([P, sets], FP32, name="total")
+            nc.vector.tensor_reduce(out=total[:], in_=shifted[:], axis=AXIS.X, op=ALU.add)
+            nc.vector.reciprocal(out=total[:], in_=total[:])
+            nc.vector.tensor_tensor(
+                out=result,
+                in0=shifted[:],
+                in1=total[:].unsqueeze(2).to_broadcast([P, sets, TOKENS]),
+                op=ALU.mult,
+            )
+
+        def keep_own_group(k):
+            even_part = work.tile([P, OCTETS, TOKENS], FP32)
+            nc.vector.tensor_scalar(
+                out=even_part[:], in0=two_groups[k][:, :, 0, :], scalar1=parity[:, 0:1], scalar2=None, op0=ALU.mult
+            )
+            nc.vector.scalar_tensor_tensor(
+                out=logits_t[:, :, k, :],
+                in0=two_groups[k][:, :, 1, :],
+                scalar=parity[:, 1:2],
+                in1=even_part[:],
+                op0=ALU.mult,
+                op1=ALU.add,
+            )
+            powers[k] = softmax_start(logits_t[:, :, k, :], OCTETS)
+
+        def exponentiate(k):
+            nc.scalar.activation(out=powers[k][:], in_=powers[k][:], func=ACT.Exp)
+
+        def finish_disp(k):
+            softmax_end(powers[k], disp_t[:, :, k, :], OCTETS)
+
+        def at(stage, index, count):
+            if 0 <= index < count:
+                stage(index)
+
+        def at_expert(stage, step, lag):
+            k, rest = divmod(step - lag, INNER)
+            if rest == 0:
+                at(stage, k, OUTER)
+
+        for c in range(PREFETCH):
+            load_chunk(c)
+        for first in range(0, MEAN_TILES, 2):
+            bank = transpose_two(mean_words, first)
+            nc.scalar.copy(
+                out=mean_slots[:, first : first + 2],
+                in_=bank[:].rearrange("p a u (b k m) -> p a b k m u", k=OUTER, m=SEGMENTS),
+            )
+
+        for step in range(LAST_STEP + 1):
+            if step % 2 == 0:
+                at(load_yn, step // 2, OCTETS)
+            at(load_chunk, step + PREFETCH, CHUNKS)
+            at(find_norm_factor, step - SQUARE_LAG, CHUNKS)
+            at(regroup, step, CHUNKS)
+            if step == 0:
+                quantise_means()
+            at(multiply_transposed, step - SPREAD_LAG, CHUNKS)
+            at(quantise_chunk, step - QUANTISE_LAG, CHUNKS)
+            at(spread_norm_factor, step - SQUARE_LAG, CHUNKS)
+            at(normalise, step - NORMALISE_LAG, CHUNKS)
+            for b in range(2):
+                at(copy_yn, 2 * (step - 1 - YN_FIRST_STEP) + b, YN_BANKS)
+            for b in range(2):
+                at(transpose_yn, 2 * (step - YN_FIRST_STEP) + b, YN_BANKS)
+            at(quantise_yn, step - YN_QUANTISE_STEP, OUTER // 2)
+            at_expert(quantise_slots, step, SLOTS_LAG)
+            at_expert(multiply_slots_and_tokens, step, LOGITS_LAG)
+            at_expert(copy_quadrants, step, LOGITS_LAG + 1)
+            at_expert(keep_own_group, step, LOGITS_LAG + 2)
+            at_expert(exponentiate, step, LOGITS_LAG + 3)
+            at_expert(finish_disp, step, LOGITS_LAG + 4)
+
+        def transpose_octets(source):
+            bank = psum.tile([P, OCTETS, P], FP32, tag="bank")
+            for i in range(OCTETS):
+                nc.tensor.transpose(bank[:, i, :], source[:, i].rearrange("p k s -> p (k s)"), ident[:])
+            return bank
+
+        logits_bank = transpose_octets(logits_t)
+        comb_powers = softmax_start(logits_bank[:].rearrange("p i (g q) -> p (i g) q", q=SLOTS), GROUPS)
+        nc.scalar.activation(out=comb_powers[:], in_=comb_powers[:], func=ACT.Exp)
+
+        disp_bank = transpose_octets(disp_t)
+        disp = work.tile([P, GROUPS, SLOTS], FP32)
+        nc.scalar.copy(out=disp[:], in_=disp_bank[:].rearrange("p i (g q) -> p (i g) q", q=SLOTS))
+        nc.sync.dma_start(out=out_0.rearrange("b g k s q -> (k s) (b g) q"), in_=disp[:])
+
+        comb = work.tile([P, GROUPS, SLOTS], FP32)
+        softmax_end(comb_powers, comb[:], GROUPS)
+        nc.sync.dma_start(out=out_1.rearrange("b g k s q -> (k s) (b g) q"), in_=comb[:])

@@ -35,9 +35,10 @@ VECTOR_WORDS = 60
 PREFETCH = 6
 QUANTISE_LAG = 1
 SQUARE_LAG = 2
-SPREAD_LAG = 3
-NORMALISE_LAG = 4
-SLOTS_LAG = 8
+FACTOR_LAG = 4
+SPREAD_LAG = 5
+NORMALISE_LAG = 6
+SLOTS_LAG = 10
 LOGITS_LAG = 14
 YN_FIRST_STEP = 4
 YN_QUANTISE_STEP = YN_FIRST_STEP + YN_BANKS // 2 + 1
@@ -55,7 +56,7 @@ def tile_hierarchicalsoftmoe2dblock_pb_kernel(tc, yn, means, w_slot2, out_0, out
         grouped_pool = ctx.enter_context(tc.tile_pool(name="grouped_pool", bufs=3))
         codes_pool = ctx.enter_context(tc.tile_pool(name="codes_pool", bufs=SPREAD_LAG + 2))
         work = ctx.enter_context(tc.tile_pool(name="work", bufs=2))
-        small = ctx.enter_context(tc.tile_pool(name="small", bufs=4))
+        small = ctx.enter_context(tc.tile_pool(name="small", bufs=6))
         psum = ctx.enter_context(tc.psum_pool(name="psum", bufs=2))
 
         ident = keep.tile([P, P], FP32)
@@ -316,7 +317,7 @@ def tile_hierarchicalsoftmoe2dblock_pb_kernel(tc, yn, means, w_slot2, out_0, out
                 quantise_means()
             at(multiply_transposed, step - SPREAD_LAG, CHUNKS)
             at(quantise_chunk, step - QUANTISE_LAG, CHUNKS)
-            at(spread_norm_factor, step - SQUARE_LAG, CHUNKS)
+            at(spread_norm_factor, step - FACTOR_LAG, CHUNKS)
             at(normalise, step - NORMALISE_LAG, CHUNKS)
             for b in range(2):
                 at(copy_yn, 2 * (step - 1 - YN_FIRST_STEP) + b, YN_BANKS)

@@ -32,17 +32,22 @@ YN_BANKS = GROUPS // 2
 
 VECTOR_WORDS = 60
 
-PREFETCH = 6
+FIRST_LOADS = 2
+W_BUFFERS = 8
 QUANTISE_LAG = 1
-SQUARE_LAG = 2
-FACTOR_LAG = 4
-SPREAD_LAG = 5
-NORMALISE_LAG = 6
-SLOTS_LAG = 10
-LOGITS_LAG = 14
-YN_FIRST_STEP = 4
-YN_QUANTISE_STEP = YN_FIRST_STEP + YN_BANKS // 2 + 1
-LAST_STEP = INNER * (OUTER - 1) + LOGITS_LAG + 4
+ROWS_LAG = 2
+SQUARE_LAG = 3
+COLUMNS_LAG = 9
+NORMALISE_LAG = 10
+FACTOR_LAG = INNER - 1 + SQUARE_LAG
+SPREAD_LAG = FACTOR_LAG + 2
+SLOTS_LAG = INNER + NORMALISE_LAG
+LOGITS_LAG = 20
+HALF = OUTER // 2
+OWN_GROUP_LAG = INNER * (HALF - 1) + LOGITS_LAG + 5
+YN_FIRST_STEP = 2
+YN_QUANTISE_STEP = YN_FIRST_STEP + YN_BANKS + 1
+LAST_STEP = INNER * HALF + OWN_GROUP_LAG + 2
 
 FLOPS = 2 * OUTER * ROWS * D * INNER * D + 2 * GROUPS * OUTER * TOKENS * SLOTS * D
 
@@ -52,9 +57,9 @@ def tile_hierarchicalsoftmoe2dblock_pb_kernel(tc, yn, means, w_slot2, out_0, out
     with ExitStack() as ctx:
         ctx.enter_context(tc.manual_schedule())
         keep = ctx.enter_context(tc.tile_pool(name="keep", bufs=1))
-        w_pool = ctx.enter_context(tc.tile_pool(name="w_pool", bufs=PREFETCH + 2))
+        w_pool = ctx.enter_context(tc.tile_pool(name="w_pool", bufs=W_BUFFERS))
         grouped_pool = ctx.enter_context(tc.tile_pool(name="grouped_pool", bufs=3))
-        codes_pool = ctx.enter_context(tc.tile_pool(name="codes_pool", bufs=SPREAD_LAG + 2))
+        codes_pool = ctx.enter_context(tc.tile_pool(name="codes_pool", bufs=COLUMNS_LAG + 1))
         work = ctx.enter_context(tc.tile_pool(name="work", bufs=2))
         small = ctx.enter_context(tc.tile_pool(name="small", bufs=6))
         psum = ctx.enter_context(tc.psum_pool(name="psum", bufs=2))
@@ -68,7 +73,7 @@ def tile_hierarchicalsoftmoe2dblock_pb_kernel(tc, yn, means, w_slot2, out_0, out
             axis=AXIS.XY,
             op=ALU.add,
         )
-        minus_half = keep.tile([P, 1], FP32)
+        minus_half = keep.tile([P, INNER], FP32)
         nc.vector.memset(minus_half[:], -0.5)
 
         mean_raw = keep.tile([P, MEAN_TILES, D], BF16)
@@ -81,12 +86,13 @@ def tile_hierarchicalsoftmoe2dblock_pb_kernel(tc, yn, means, w_slot2, out_0, out
         yn_scales = keep.tile([P, OUTER, GROUPS * TOKENS], U8, align_bytes=64)
         se2_codes = keep.tile([P, OUTER, GROUPS * SLOTS], U32, align_bytes=64)
         se2_scales = keep.tile([P, OUTER, GROUPS * SLOTS], U8, align_bytes=64)
+        two_groups = keep.tile([P, 2, OCTETS, HALF, 2, TOKENS], FP32)
         logits_t = keep.tile([P, OCTETS, OUTER, TOKENS], FP32)
         disp_t = keep.tile([P, OCTETS, OUTER, TOKENS], FP32)
 
         w_raw, grouped, w_codes, w_scales = {}, {}, {}, {}
-        se_rows, norm_factor, spread_bank, spread, se_cols, se2_grouped = {}, {}, {}, {}, {}, {}
-        yn_bank, all_pairs, two_groups, powers = {}, {}, {}, {}
+        se_rows, sum_squares, norm_factor, spread_bank, spread = {}, {}, {}, {}, {}
+        se_cols, se2_grouped, yn_bank, all_pairs, powers = {}, {}, {}, {}, {}
 
         def transpose_two(words, first):
             bank = psum.tile([P, 2, 2, P], FP32, tag="bank")
@@ -128,12 +134,11 @@ def tile_hierarchicalsoftmoe2dblock_pb_kernel(tc, yn, means, w_slot2, out_0, out
                 in_=yn_bank[b][:].rearrange("p g u (k s) -> p g k s u", k=OUTER),
             )
 
-        def quantise_yn(pair):
-            two = slice(2 * pair, 2 * pair + 2)
+        def quantise_yn(k):
             nc.vector.quantize_mx(
-                out=yn_codes[:, two, :].rearrange("p k c -> p (k c)").bitcast(FP8X4),
-                scales=yn_scales[:, two, :].rearrange("p k c -> p (k c)"),
-                in_=yn_grouped[:, two].rearrange("p k g s t -> p (k g s t)"),
+                out=yn_codes[:, k, :].bitcast(FP8X4),
+                scales=yn_scales[:, k, :],
+                in_=yn_grouped[:, k].rearrange("p g s t -> p (g s t)"),
             )
 
         def load_chunk(c):
@@ -157,6 +162,8 @@ def tile_hierarchicalsoftmoe2dblock_pb_kernel(tc, yn, means, w_slot2, out_0, out
                 scales=w_scales[c][:],
                 in_=grouped[c][:].rearrange("p t w j -> p (t w j)"),
             )
+
+        def multiply_rows(c):
             se_rows[c] = psum.tile([P, D], FP32, name="se_rows")
             nc.tensor.matmul_mx(
                 out=se_rows[c][:],
@@ -168,24 +175,16 @@ def tile_hierarchicalsoftmoe2dblock_pb_kernel(tc, yn, means, w_slot2, out_0, out
                 stop=True,
             )
 
-        def find_norm_factor(c):
+        def square_rows(c):
+            k, e = divmod(c, INNER)
+            if e == 0:
+                sum_squares[k] = small.tile([P, INNER], FP32, name="sum_squares")
             squares = work.tile([P, D], BF16)
-            sum_squares = small.tile([P, 1], FP32)
-            nc.scalar.activation(out=squares[:], in_=se_rows[c][:], func=ACT.Square, accum_out=sum_squares[:])
-            mean_square = small.tile([P, 1], FP32)
-            nc.gpsimd.tensor_scalar(
-                out=mean_square[:], in0=sum_squares[:], scalar1=1.0 / D, scalar2=EPS / D, op0=ALU.mult, op1=ALU.add
+            nc.scalar.activation(
+                out=squares[:], in_=se_rows[c][:], func=ACT.Square, accum_out=sum_squares[k][:, e : e + 1]
             )
-            norm_factor[c] = small.tile([P, 1], FP32, name="norm_factor")
-            nc.gpsimd.tensor_tensor(out=norm_factor[c][:], in0=mean_square[:], in1=minus_half[:], op=ALU.pow)
-
-        def spread_norm_factor(c):
-            spread_bank[c] = psum.tile([P, ROWS], FP32, name="spread_bank")
-            nc.tensor.transpose(spread_bank[c][:], norm_factor[c][:].to_broadcast([P, P]), ident[:])
 
         def multiply_transposed(c):
-            spread[c] = work.tile([P, ROWS], FP32, name="spread", bufs=3)
-            nc.scalar.copy(out=spread[c][:], in_=spread_bank[c][:])
             se_cols[c] = psum.tile([P, PACK, ROWS], FP32, name="se_cols")
             for t in range(PACK):
                 block = slice(t * P, (t + 1) * P)
@@ -208,12 +207,31 @@ def tile_hierarchicalsoftmoe2dblock_pb_kernel(tc, yn, means, w_slot2, out_0, out
             nc.vector.tensor_tensor(
                 out=se2_grouped[k][:, :, e, :, :],
                 in0=se_cols[c][:].rearrange("p t (g m) -> p g m t", m=SEGMENTS),
-                in1=spread[c][:]
+                in1=spread[k][:, e, :]
                 .rearrange("p (g m) -> p g m", m=SEGMENTS)
                 .unsqueeze(3)
                 .to_broadcast([P, GROUPS, SEGMENTS, PACK]),
                 op=ALU.mult,
             )
+
+        def find_norm_factor(k):
+            mean_square = small.tile([P, INNER], FP32)
+            nc.gpsimd.tensor_scalar(
+                out=mean_square[:], in0=sum_squares[k][:], scalar1=1.0 / D, scalar2=EPS / D, op0=ALU.mult, op1=ALU.add
+            )
+            norm_factor[k] = small.tile([P, INNER], FP32, name="norm_factor")
+            nc.gpsimd.tensor_tensor(out=norm_factor[k][:], in0=mean_square[:], in1=minus_half[:], op=ALU.pow)
+
+        def spread_norm_factor(k):
+            spread_bank[k] = psum.tile([P, INNER, ROWS], FP32, name="spread_bank")
+            for e in range(INNER):
+                nc.tensor.transpose(
+                    spread_bank[k][:, e, :], norm_factor[k][:, e : e + 1].to_broadcast([P, P]), ident[:]
+                )
+
+        def copy_spread(k):
+            spread[k] = work.tile([P, INNER, ROWS], FP32, name="spread")
+            nc.scalar.copy(out=spread[k][:], in_=spread_bank[k][:])
 
         def quantise_slots(k):
             nc.vector.quantize_mx(
@@ -236,58 +254,60 @@ def tile_hierarchicalsoftmoe2dblock_pb_kernel(tc, yn, means, w_slot2, out_0, out
                     stop=True,
                 )
 
-        def copy_quadrants(k):
-            two_groups[k] = work.tile([P, OCTETS, 2, TOKENS], FP32, name="two_groups")
-            for quadrant in range(4):
-                rows = slice(32 * quadrant, 32 * quadrant + 32)
-                nc.scalar.copy(
-                    out=two_groups[k][rows],
-                    in_=all_pairs[k][rows, :, 32 * quadrant : 32 * quadrant + 32].rearrange(
-                        "p i (h s) -> p i h s", h=2
-                    ),
-                )
+        def copy_quadrant(k, quadrant):
+            rows = slice(32 * quadrant, 32 * quadrant + 32)
+            nc.scalar.copy(
+                out=two_groups[rows, k // HALF, :, k % HALF],
+                in_=all_pairs[k][rows, :, 32 * quadrant : 32 * quadrant + 32].rearrange(
+                    "p i (h s) -> p i h s", h=2
+                ),
+            )
 
         def softmax_start(logits, sets):
-            shape = [P, sets, TOKENS]
-            top = small.tile([P, sets], FP32, name="top")
+            top = small.tile([P] + sets, FP32, name="top")
             nc.vector.tensor_reduce(out=top[:], in_=logits, axis=AXIS.X, op=ALU.max)
-            shifted = work.tile(shape, FP32, name="shifted", bufs=3)
+            shifted = work.tile([P] + sets + [TOKENS], FP32, name="shifted")
             nc.vector.tensor_tensor(
-                out=shifted[:], in0=logits, in1=top[:].unsqueeze(2).to_broadcast(shape), op=ALU.subtract
+                out=shifted[:],
+                in0=logits,
+                in1=top[:].unsqueeze(3).to_broadcast([P] + sets + [TOKENS]),
+                op=ALU.subtract,
             )
             return shifted
 
-        def softmax_end(shifted, result, sets):
-            total = small.tile([P, sets], FP32, name="total")
-            nc.vector.tensor_reduce(out=total[:], in_=shifted[:], axis=AXIS.X, op=ALU.add)
+        def softmax_end(exponentials, result, sets):
+            total = small.tile([P] + sets, FP32, name="total")
+            nc.vector.tensor_reduce(out=total[:], in_=exponentials[:], axis=AXIS.X, op=ALU.add)
             nc.vector.reciprocal(out=total[:], in_=total[:])
             nc.vector.tensor_tensor(
                 out=result,
-                in0=shifted[:],
-                in1=total[:].unsqueeze(2).to_broadcast([P, sets, TOKENS]),
+                in0=exponentials[:],
+                in1=total[:].unsqueeze(3).to_broadcast([P] + sets + [TOKENS]),
                 op=ALU.mult,
             )
 
-        def keep_own_group(k):
-            even_part = work.tile([P, OCTETS, TOKENS], FP32)
+        def keep_own_group(half):
+            experts = slice(half * HALF, (half + 1) * HALF)
+            even_part = work.tile([P, OCTETS, HALF, TOKENS], FP32)
             nc.vector.tensor_scalar(
-                out=even_part[:], in0=two_groups[k][:, :, 0, :], scalar1=parity[:, 0:1], scalar2=None, op0=ALU.mult
+                out=even_part[:], in0=two_groups[:, half, :, :, 0, :], scalar1=parity[:, 0:1], scalar2=None, op0=ALU.mult
             )
             nc.vector.scalar_tensor_tensor(
-                out=logits_t[:, :, k, :],
-                in0=two_groups[k][:, :, 1, :],
+                out=logits_t[:, :, experts, :],
+                in0=two_groups[:, half, :, :, 1, :],
                 scalar=parity[:, 1:2],
                 in1=even_part[:],
                 op0=ALU.mult,
                 op1=ALU.add,
             )
-            powers[k] = softmax_start(logits_t[:, :, k, :], OCTETS)
+            powers[half] = softmax_start(logits_t[:, :, experts, :], [OCTETS, HALF])
 
-        def exponentiate(k):
-            nc.scalar.activation(out=powers[k][:], in_=powers[k][:], func=ACT.Exp)
+        def exponentiate(half):
+            nc.scalar.activation(out=powers[half][:], in_=powers[half][:], func=ACT.Exp)
 
-        def finish_disp(k):
-            softmax_end(powers[k], disp_t[:, :, k, :], OCTETS)
+        def finish_disp(half):
+            experts = slice(half * HALF, (half + 1) * HALF)
+            softmax_end(powers[half], disp_t[:, :, experts, :], [OCTETS, HALF])
 
         def at(stage, index, count):
             if 0 <= index < count:
@@ -298,7 +318,12 @@ def tile_hierarchicalsoftmoe2dblock_pb_kernel(tc, yn, means, w_slot2, out_0, out
             if rest == 0:
                 at(stage, k, OUTER)
 
-        for c in range(PREFETCH):
+        def at_half(stage, step, lag):
+            half, rest = divmod(step - lag, INNER * HALF)
+            if rest == 0:
+                at(stage, half, 2)
+
+        for c in range(FIRST_LOADS):
             load_chunk(c)
         for first in range(0, MEAN_TILES, 2):
             bank = transpose_two(mean_words, first)
@@ -308,28 +333,30 @@ def tile_hierarchicalsoftmoe2dblock_pb_kernel(tc, yn, means, w_slot2, out_0, out
             )
 
         for step in range(LAST_STEP + 1):
-            if step % 2 == 0:
-                at(load_yn, step // 2, OCTETS)
-            at(load_chunk, step + PREFETCH, CHUNKS)
-            at(find_norm_factor, step - SQUARE_LAG, CHUNKS)
+            if step % INNER == 0:
+                at(load_yn, step // INNER, OCTETS)
+            at(load_chunk, step + FIRST_LOADS, CHUNKS)
+            at(square_rows, step - SQUARE_LAG, CHUNKS)
+            at_expert(find_norm_factor, step, FACTOR_LAG)
             at(regroup, step, CHUNKS)
             if step == 0:
                 quantise_means()
-            at(multiply_transposed, step - SPREAD_LAG, CHUNKS)
-            at(quantise_chunk, step - QUANTISE_LAG, CHUNKS)
-            at(spread_norm_factor, step - FACTOR_LAG, CHUNKS)
-            at(normalise, step - NORMALISE_LAG, CHUNKS)
-            for b in range(2):
-                at(copy_yn, 2 * (step - 1 - YN_FIRST_STEP) + b, YN_BANKS)
-            for b in range(2):
-                at(transpose_yn, 2 * (step - YN_FIRST_STEP) + b, YN_BANKS)
-            at(quantise_yn, step - YN_QUANTISE_STEP, OUTER // 2)
-            at_expert(quantise_slots, step, SLOTS_LAG)
+            at(multiply_rows, step - ROWS_LAG, CHUNKS)
+            at(multiply_transposed, step - COLUMNS_LAG, CHUNKS)
             at_expert(multiply_slots_and_tokens, step, LOGITS_LAG)
-            at_expert(copy_quadrants, step, LOGITS_LAG + 1)
-            at_expert(keep_own_group, step, LOGITS_LAG + 2)
-            at_expert(exponentiate, step, LOGITS_LAG + 3)
-            at_expert(finish_disp, step, LOGITS_LAG + 4)
+            at_expert(spread_norm_factor, step, SPREAD_LAG)
+            at(quantise_chunk, step - QUANTISE_LAG, CHUNKS)
+            at_expert(copy_spread, step, SPREAD_LAG + 1)
+            at(normalise, step - NORMALISE_LAG, CHUNKS)
+            at(copy_yn, step - 1 - YN_FIRST_STEP, YN_BANKS)
+            at(transpose_yn, step - YN_FIRST_STEP, YN_BANKS)
+            at(quantise_yn, step - YN_QUANTISE_STEP, OUTER)
+            at_expert(quantise_slots, step, SLOTS_LAG)
+            for quadrant in range(4):
+                at_expert(lambda k: copy_quadrant(k, quadrant), step, LOGITS_LAG + 1 + quadrant)
+            at_half(keep_own_group, step, OWN_GROUP_LAG)
+            at_half(exponentiate, step, OWN_GROUP_LAG + 1)
+            at_half(finish_disp, step, OWN_GROUP_LAG + 2)
 
         def transpose_octets(source):
             bank = psum.tile([P, OCTETS, P], FP32, tag="bank")
@@ -338,14 +365,16 @@ def tile_hierarchicalsoftmoe2dblock_pb_kernel(tc, yn, means, w_slot2, out_0, out
             return bank
 
         logits_bank = transpose_octets(logits_t)
-        comb_powers = softmax_start(logits_bank[:].rearrange("p i (g q) -> p (i g) q", q=SLOTS), GROUPS)
+        comb_powers = softmax_start(logits_bank[:].rearrange("p i (g q) -> p i g q", q=SLOTS), [OCTETS, OCTET])
         nc.scalar.activation(out=comb_powers[:], in_=comb_powers[:], func=ACT.Exp)
 
         disp_bank = transpose_octets(disp_t)
-        disp = work.tile([P, GROUPS, SLOTS], FP32)
+        disp = work.tile([P, GROUPS, SLOTS], FP32, bufs=1)
         nc.scalar.copy(out=disp[:], in_=disp_bank[:].rearrange("p i (g q) -> p (i g) q", q=SLOTS))
         nc.sync.dma_start(out=out_0.rearrange("b g k s q -> (k s) (b g) q"), in_=disp[:])
 
-        comb = work.tile([P, GROUPS, SLOTS], FP32)
-        softmax_end(comb_powers, comb[:], GROUPS)
-        nc.sync.dma_start(out=out_1.rearrange("b g k s q -> (k s) (b g) q"), in_=comb[:])
+        comb = work.tile([P, OCTETS, OCTET, SLOTS], FP32, bufs=1)
+        softmax_end(comb_powers, comb[:], [OCTETS, OCTET])
+        nc.sync.dma_start(
+            out=out_1.rearrange("b g k s q -> (k s) (b g) q"), in_=comb[:].rearrange("p i g q -> p (i g) q")
+        )

@@ -30,24 +30,30 @@ CHUNKS = OUTER * INNER
 MEAN_TILES = GROUPS * OUTER * SEGMENTS // P
 YN_BANKS = GROUPS // 2
 
-VECTOR_WORDS = 60
+VECTOR_COLUMNS = 384
+EARLY_VECTOR_COLUMNS = 336
+LATE_VECTOR_COLUMNS = 320
+LATE_STEPS = 6
+QUADRANT_LAG = 1
 
 FIRST_LOADS = 2
 W_BUFFERS = 8
 QUANTISE_LAG = 1
+MEANS_STEP = 2
 ROWS_LAG = 2
-SQUARE_LAG = 3
-COLUMNS_LAG = 9
-NORMALISE_LAG = 10
+SQUARE_LAG = ROWS_LAG + 1
+AGAIN_LAG = ROWS_LAG + 6
+SCALE_LAG = AGAIN_LAG + 1
+TURN_LAG = SCALE_LAG + 1
+GROUP_LAG = TURN_LAG + 1
+MEANS_LOAD_STEP = 0
 FACTOR_LAG = INNER - 1 + SQUARE_LAG
-SPREAD_LAG = FACTOR_LAG + 2
-SLOTS_LAG = INNER + NORMALISE_LAG
-LOGITS_LAG = 20
-HALF = OUTER // 2
-OWN_GROUP_LAG = INNER * (HALF - 1) + LOGITS_LAG + 5
-YN_FIRST_STEP = 2
+SLOTS_LAG = INNER + GROUP_LAG
+PAIRS = OUTER // 2
+YN_LOAD_STEP = 4
+YN_FIRST_STEP = 6
 YN_QUANTISE_STEP = YN_FIRST_STEP + YN_BANKS + 1
-LAST_STEP = INNER * HALF + OWN_GROUP_LAG + 2
+LAST_STEP = INNER * (OUTER - 1) + SLOTS_LAG + 3 + 5
 
 FLOPS = 2 * OUTER * ROWS * D * INNER * D + 2 * GROUPS * OUTER * TOKENS * SLOTS * D
 
@@ -59,7 +65,7 @@ def tile_hierarchicalsoftmoe2dblock_pb_kernel(tc, yn, means, w_slot2, out_0, out
         keep = ctx.enter_context(tc.tile_pool(name="keep", bufs=1))
         w_pool = ctx.enter_context(tc.tile_pool(name="w_pool", bufs=W_BUFFERS))
         grouped_pool = ctx.enter_context(tc.tile_pool(name="grouped_pool", bufs=3))
-        codes_pool = ctx.enter_context(tc.tile_pool(name="codes_pool", bufs=COLUMNS_LAG + 1))
+        codes_pool = ctx.enter_context(tc.tile_pool(name="codes_pool", bufs=AGAIN_LAG + 1))
         work = ctx.enter_context(tc.tile_pool(name="work", bufs=2))
         small = ctx.enter_context(tc.tile_pool(name="small", bufs=6))
         psum = ctx.enter_context(tc.psum_pool(name="psum", bufs=2))
@@ -75,6 +81,8 @@ def tile_hierarchicalsoftmoe2dblock_pb_kernel(tc, yn, means, w_slot2, out_0, out
         )
         minus_half = keep.tile([P, INNER], FP32)
         nc.vector.memset(minus_half[:], -0.5)
+        warm = keep.tile([P, 1], FP32)
+        nc.scalar.activation(out=warm[:], in_=minus_half[:, 0:1], func=ACT.Exp)
 
         mean_raw = keep.tile([P, MEAN_TILES, D], BF16)
         mean_grouped = keep.tile([P, OUTER, ROWS, PACK], BF16, align_bytes=64)
@@ -86,24 +94,23 @@ def tile_hierarchicalsoftmoe2dblock_pb_kernel(tc, yn, means, w_slot2, out_0, out
         yn_scales = keep.tile([P, OUTER, GROUPS * TOKENS], U8, align_bytes=64)
         se2_codes = keep.tile([P, OUTER, GROUPS * SLOTS], U32, align_bytes=64)
         se2_scales = keep.tile([P, OUTER, GROUPS * SLOTS], U8, align_bytes=64)
-        two_groups = keep.tile([P, 2, OCTETS, HALF, 2, TOKENS], FP32)
-        logits_t = keep.tile([P, OCTETS, OUTER, TOKENS], FP32)
-        disp_t = keep.tile([P, OCTETS, OUTER, TOKENS], FP32)
+        two_groups = keep.tile([P, PAIRS, OCTETS, 2, 2, TOKENS], FP32)
+        logits_t = keep.tile([P, PAIRS, OCTETS, 2, TOKENS], FP32)
+        disp_t = keep.tile([P, PAIRS, OCTETS, 2, TOKENS], FP32)
 
         w_raw, grouped, w_codes, w_scales = {}, {}, {}, {}
         se_rows, sum_squares, norm_factor, spread_bank, spread = {}, {}, {}, {}, {}
-        se_cols, se2_grouped, yn_bank, all_pairs, powers = {}, {}, {}, {}, {}
+        se_again, se2_rows, slots_bank, se2_grouped, yn_bank, all_pairs = {}, {}, {}, {}, {}, {}
+        even_part, top, powers, total, bank_of, result = {}, {}, {}, {}, {}, {}
 
-        def transpose_two(words, first):
-            bank = psum.tile([P, 2, 2, P], FP32, tag="bank")
+        def transpose_two(words, first, tag, bufs):
+            bank = psum.tile([P, 2, 2, P], FP32, tag=tag, bufs=bufs)
             for a in range(2):
                 for u in range(2):
                     nc.tensor.transpose(bank[:, a, u, :], words[:, first + a, u, :], ident[:])
             return bank
 
         mean_rows = means.flatten_outer_dims().rearrange("(a p) d -> p a d", p=P)
-        for half in (slice(0, MEAN_TILES // 2), slice(MEAN_TILES // 2, MEAN_TILES)):
-            nc.sync.dma_start(out=mean_raw[:, half, :], in_=mean_rows[:, half, :])
         mean_words = mean_raw[:].bitcast(FP32).rearrange("p a (w u) -> p a u w", u=2)
         mean_slots = mean_grouped[:].bitcast(FP32).rearrange(
             "p k (a b m) u -> p a b k m u", a=MEAN_TILES, m=SEGMENTS
@@ -125,7 +132,7 @@ def tile_hierarchicalsoftmoe2dblock_pb_kernel(tc, yn, means, w_slot2, out_0, out
             nc.sync.dma_start(out=yn_raw[:, some, :], in_=yn_rows[:, some, :])
 
         def transpose_yn(b):
-            yn_bank[b] = transpose_two(yn_words, 2 * b)
+            yn_bank[b] = transpose_two(yn_words, 2 * b, "turned", 1)
 
         def copy_yn(b):
             copy = nc.scalar.copy if b % 2 == 0 else nc.vector.tensor_copy
@@ -148,11 +155,13 @@ def tile_hierarchicalsoftmoe2dblock_pb_kernel(tc, yn, means, w_slot2, out_0, out
             nc.sync.dma_start(out=w_raw[c][:], in_=rows[:, :, e * D : (e + 1) * D])
 
         def regroup(c):
-            grouped[c] = grouped_pool.tile([P, PACK, P, PACK], BF16, name="grouped", align_bytes=64)
-            to_words = grouped[c][:].rearrange("p t w j -> p w j t")
-            from_rows = w_raw[c][:].rearrange("p j (w t) -> p w j t", t=PACK)
-            nc.vector.tensor_copy(out=to_words[:, :VECTOR_WORDS], in_=from_rows[:, :VECTOR_WORDS])
-            nc.scalar.copy(out=to_words[:, VECTOR_WORDS:], in_=from_rows[:, VECTOR_WORDS:])
+            grouped[c] = grouped_pool.tile([P, D, PACK], BF16, name="grouped", align_bytes=64)
+            to_words = grouped[c][:].rearrange("p (n i) j -> p n j i", i=4)
+            from_rows = w_raw[c][:].rearrange("p j (n i) -> p n j i", i=4)
+            fours = (EARLY_VECTOR_COLUMNS if c < SCALE_LAG else LATE_VECTOR_COLUMNS if c >= CHUNKS - LATE_STEPS else VECTOR_COLUMNS) // 4
+            nc.vector.tensor_copy(out=to_words[:, :fours], in_=from_rows[:, :fours])
+            if fours < D // 4:
+                nc.scalar.copy(out=to_words[:, fours:], in_=from_rows[:, fours:])
 
         def quantise_chunk(c):
             w_codes[c] = codes_pool.tile([P, D], U32, name="w_codes", align_bytes=64)
@@ -160,7 +169,7 @@ def tile_hierarchicalsoftmoe2dblock_pb_kernel(tc, yn, means, w_slot2, out_0, out
             nc.vector.quantize_mx(
                 out=w_codes[c][:].bitcast(FP8X4),
                 scales=w_scales[c][:],
-                in_=grouped[c][:].rearrange("p t w j -> p (t w j)"),
+                in_=grouped[c][:].rearrange("p n j -> p (n j)"),
             )
 
         def multiply_rows(c):
@@ -184,34 +193,40 @@ def tile_hierarchicalsoftmoe2dblock_pb_kernel(tc, yn, means, w_slot2, out_0, out
                 out=squares[:], in_=se_rows[c][:], func=ACT.Square, accum_out=sum_squares[k][:, e : e + 1]
             )
 
-        def multiply_transposed(c):
-            se_cols[c] = psum.tile([P, PACK, ROWS], FP32, name="se_cols")
-            for t in range(PACK):
-                block = slice(t * P, (t + 1) * P)
-                nc.tensor.matmul_mx(
-                    out=se_cols[c][:, t, :],
-                    lhsT=w_codes[c][:, block].bitcast(FP8X4),
-                    lhsT_scale=w_scales[c][:, block],
-                    rhs=mean_codes[:, c // INNER, :].bitcast(FP8X4),
-                    rhs_scale=mean_scales[:, c // INNER, :],
-                    start=True,
-                    stop=True,
-                )
+        def multiply_again(c):
+            se_again[c] = psum.tile([P, D], FP32, name="se_again")
+            nc.tensor.matmul_mx(
+                out=se_again[c][:],
+                lhsT=mean_codes[:, c // INNER, :].bitcast(FP8X4),
+                lhsT_scale=mean_scales[:, c // INNER, :],
+                rhs=w_codes[c][:].bitcast(FP8X4),
+                rhs_scale=w_scales[c][:],
+                start=True,
+                stop=True,
+            )
 
         def normalise(c):
             k, e = divmod(c, INNER)
-            if e == 0:
+            se2_rows[c] = work.tile([P, D], BF16, name="se2_rows", bufs=3)
+            nc.scalar.activation(out=se2_rows[c][:], in_=se_again[c][:], func=ACT.Copy, scale=norm_factor[k][:, e : e + 1])
+
+        def turn_slots(c):
+            if c % 2 == 0:
+                slots_bank[c // 2] = psum.tile([P, 2, 2, P], FP32, name="slots_bank")
+            words = se2_rows[c][:].bitcast(FP32).rearrange("p (w u) -> p u w", u=2)
+            for u in range(2):
+                nc.tensor.transpose(slots_bank[c // 2][:, c % 2, u, :], words[:, u, :], ident[:])
+
+        def group_slots(two):
+            k, first = divmod(2 * two, INNER)
+            if first == 0:
                 se2_grouped[k] = work.tile(
                     [P, GROUPS, INNER, SEGMENTS, PACK], BF16, name="se2_grouped", align_bytes=64
                 )
-            nc.vector.tensor_tensor(
-                out=se2_grouped[k][:, :, e, :, :],
-                in0=se_cols[c][:].rearrange("p t (g m) -> p g m t", m=SEGMENTS),
-                in1=spread[k][:, e, :]
-                .rearrange("p (g m) -> p g m", m=SEGMENTS)
-                .unsqueeze(3)
-                .to_broadcast([P, GROUPS, SEGMENTS, PACK]),
-                op=ALU.mult,
+            copy = nc.scalar.copy if two % 2 == 0 else nc.vector.tensor_copy
+            copy(
+                out=se2_grouped[k][:].bitcast(FP32)[:, :, first : first + 2, :, :],
+                in_=slots_bank[two][:].rearrange("p e u (g m) -> p g e m u", m=SEGMENTS),
             )
 
         def find_norm_factor(k):
@@ -222,17 +237,6 @@ def tile_hierarchicalsoftmoe2dblock_pb_kernel(tc, yn, means, w_slot2, out_0, out
             norm_factor[k] = small.tile([P, INNER], FP32, name="norm_factor")
             nc.gpsimd.tensor_tensor(out=norm_factor[k][:], in0=mean_square[:], in1=minus_half[:], op=ALU.pow)
 
-        def spread_norm_factor(k):
-            spread_bank[k] = psum.tile([P, INNER, ROWS], FP32, name="spread_bank")
-            for e in range(INNER):
-                nc.tensor.transpose(
-                    spread_bank[k][:, e, :], norm_factor[k][:, e : e + 1].to_broadcast([P, P]), ident[:]
-                )
-
-        def copy_spread(k):
-            spread[k] = work.tile([P, INNER, ROWS], FP32, name="spread")
-            nc.scalar.copy(out=spread[k][:], in_=spread_bank[k][:])
-
         def quantise_slots(k):
             nc.vector.quantize_mx(
                 out=se2_codes[:, k, :].bitcast(FP8X4),
@@ -241,7 +245,7 @@ def tile_hierarchicalsoftmoe2dblock_pb_kernel(tc, yn, means, w_slot2, out_0, out
             )
 
         def multiply_slots_and_tokens(k):
-            all_pairs[k] = psum.tile([P, OCTETS, P], FP32, tag="bank", name="all_pairs")
+            all_pairs[k] = psum.tile([P, OCTETS, P], FP32, name="all_pairs", bufs=1)
             for i in range(OCTETS):
                 block = slice(i * P, (i + 1) * P)
                 nc.tensor.matmul_mx(
@@ -257,57 +261,93 @@ def tile_hierarchicalsoftmoe2dblock_pb_kernel(tc, yn, means, w_slot2, out_0, out
         def copy_quadrant(k, quadrant):
             rows = slice(32 * quadrant, 32 * quadrant + 32)
             nc.scalar.copy(
-                out=two_groups[rows, k // HALF, :, k % HALF],
+                out=two_groups[rows, k // 2, :, k % 2],
                 in_=all_pairs[k][rows, :, 32 * quadrant : 32 * quadrant + 32].rearrange(
                     "p i (h s) -> p i h s", h=2
                 ),
             )
 
-        def softmax_start(logits, sets):
-            top = small.tile([P] + sets, FP32, name="top")
-            nc.vector.tensor_reduce(out=top[:], in_=logits, axis=AXIS.X, op=ALU.max)
-            shifted = work.tile([P] + sets + [TOKENS], FP32, name="shifted")
-            nc.vector.tensor_tensor(
-                out=shifted[:],
-                in0=logits,
-                in1=top[:].unsqueeze(3).to_broadcast([P] + sets + [TOKENS]),
-                op=ALU.subtract,
-            )
-            return shifted
+        DISP, COMB = 0, 1
+        SETS = {DISP: [OCTETS, 2], COMB: [OCTET]}
 
-        def softmax_end(exponentials, result, sets):
-            total = small.tile([P] + sets, FP32, name="total")
-            nc.vector.tensor_reduce(out=total[:], in_=exponentials[:], axis=AXIS.X, op=ALU.add)
-            nc.vector.reciprocal(out=total[:], in_=total[:])
-            nc.vector.tensor_tensor(
-                out=result,
-                in0=exponentials[:],
-                in1=total[:].unsqueeze(3).to_broadcast([P] + sets + [TOKENS]),
-                op=ALU.mult,
-            )
+        def spread_last(values, which):
+            sets = SETS[which]
+            return values[:].unsqueeze(len(sets) + 1).to_broadcast([P] + sets + [TOKENS])
 
-        def keep_own_group(half):
-            experts = slice(half * HALF, (half + 1) * HALF)
-            even_part = work.tile([P, OCTETS, HALF, TOKENS], FP32)
+        def logits_of(pair, which):
+            if which == DISP:
+                return logits_t[:, pair]
+            return bank_of[pair, COMB][:].rearrange("p (g q) -> p g q", q=SLOTS)
+
+        def take_even_group(pair):
+            even_part[pair] = work.tile([P, OCTETS, 2, TOKENS], FP32, name="even_part")
             nc.vector.tensor_scalar(
-                out=even_part[:], in0=two_groups[:, half, :, :, 0, :], scalar1=parity[:, 0:1], scalar2=None, op0=ALU.mult
+                out=even_part[pair][:],
+                in0=two_groups[:, pair, :, :, 0, :],
+                scalar1=parity[:, 0:1],
+                scalar2=None,
+                op0=ALU.mult,
             )
+
+        def add_odd_group(pair):
             nc.vector.scalar_tensor_tensor(
-                out=logits_t[:, :, experts, :],
-                in0=two_groups[:, half, :, :, 1, :],
+                out=logits_t[:, pair],
+                in0=two_groups[:, pair, :, :, 1, :],
                 scalar=parity[:, 1:2],
-                in1=even_part[:],
+                in1=even_part[pair][:],
                 op0=ALU.mult,
                 op1=ALU.add,
             )
-            powers[half] = softmax_start(logits_t[:, :, experts, :], [OCTETS, HALF])
 
-        def exponentiate(half):
-            nc.scalar.activation(out=powers[half][:], in_=powers[half][:], func=ACT.Exp)
+        def find_top(pair, which):
+            top[pair, which] = small.tile([P] + SETS[which], FP32, name="top")
+            nc.vector.tensor_reduce(out=top[pair, which][:], in_=logits_of(pair, which), axis=AXIS.X, op=ALU.max)
 
-        def finish_disp(half):
-            experts = slice(half * HALF, (half + 1) * HALF)
-            softmax_end(powers[half], disp_t[:, :, experts, :], [OCTETS, HALF])
+        def subtract_top(pair, which):
+            powers[pair, which] = work.tile([P] + SETS[which] + [TOKENS], FP32, name="powers", bufs=4)
+            nc.vector.tensor_tensor(
+                out=powers[pair, which][:],
+                in0=logits_of(pair, which),
+                in1=spread_last(top[pair, which], which),
+                op=ALU.subtract,
+            )
+
+        def exponentiate(pair, which):
+            nc.scalar.activation(out=powers[pair, which][:], in_=powers[pair, which][:], func=ACT.Exp)
+
+        def find_total(pair, which):
+            total[pair, which] = small.tile([P] + SETS[which], FP32, name="total")
+            nc.vector.tensor_reduce(out=total[pair, which][:], in_=powers[pair, which][:], axis=AXIS.X, op=ALU.add)
+
+        def invert_total(pair, which):
+            nc.vector.reciprocal(out=total[pair, which][:], in_=total[pair, which][:])
+
+        def divide(pair, which):
+            if which == COMB:
+                result[pair, COMB] = work.tile([P, OCTET, SLOTS], FP32, name="comb")
+            nc.vector.tensor_tensor(
+                out=disp_t[:, pair] if which == DISP else result[pair, COMB][:],
+                in0=powers[pair, which][:],
+                in1=spread_last(total[pair, which], which),
+                op=ALU.mult,
+            )
+
+        def transpose_pair(pair, which):
+            source = logits_t if which == COMB else disp_t
+            bank_of[pair, which] = psum.tile([P, P], FP32, tag="turned", name="bank_of", bufs=1)
+            nc.tensor.transpose(bank_of[pair, which][:], source[:, pair].rearrange("p i k s -> p (i k s)"), ident[:])
+
+        def copy_disp(pair):
+            result[pair, DISP] = work.tile([P, OCTET, SLOTS], FP32, name="disp")
+            nc.scalar.copy(out=result[pair, DISP][:], in_=bank_of[pair, DISP][:].rearrange("p (g q) -> p g q", q=SLOTS))
+
+        def store(pair, which):
+            out = out_0 if which == DISP else out_1
+            for b in range(OCTETS):
+                nc.sync.dma_start(
+                    out=out[b, :, 2 * pair : 2 * pair + 2].rearrange("g k s q -> (k s) g q"),
+                    in_=result[pair, which][32 * b : 32 * b + 32],
+                )
 
         def at(stage, index, count):
             if 0 <= index < count:
@@ -318,63 +358,107 @@ def tile_hierarchicalsoftmoe2dblock_pb_kernel(tc, yn, means, w_slot2, out_0, out
             if rest == 0:
                 at(stage, k, OUTER)
 
-        def at_half(stage, step, lag):
-            half, rest = divmod(step - lag, INNER * HALF)
-            if rest == 0:
-                at(stage, half, 2)
+        def logits_step(k):
+            return max(INNER * k + SLOTS_LAG, YN_QUANTISE_STEP + k) + 1
+
+        def quadrant_step(k, quadrant):
+            return logits_step(k) + (QUADRANT_LAG if k < OUTER - 1 else 1)
+
+        def pair_step(pair):
+            ready = quadrant_step(2 * pair + 1, 3) + 1
+            return ready if pair == 0 else max(ready, pair_step(pair - 1) + 5)
+
+        vector_stages = [
+            (0, take_even_group, None),
+            (0, add_odd_group, None),
+            (0, find_top, DISP),
+            (1, subtract_top, DISP),
+            (2, find_top, COMB),
+            (2, subtract_top, COMB),
+            (3, find_total, DISP),
+            (3, invert_total, DISP),
+            (3, divide, DISP),
+            (4, find_total, COMB),
+            (4, invert_total, COMB),
+            (4, divide, COMB),
+        ]
+        other_stages = [
+            (1, transpose_pair, COMB),
+            (2, exponentiate, DISP),
+            (3, exponentiate, COMB),
+            (4, transpose_pair, DISP),
+            (5, copy_disp, None),
+            (5, store, DISP),
+            (5, store, COMB),
+        ]
+
+        def due(stages, step):
+            return [
+                (stage, pair, which)
+                for pair in range(PAIRS)
+                for lag, stage, which in stages
+                if step == pair_step(pair) + lag
+            ]
+
+        def run(some):
+            for stage, pair, which in some:
+                if which is None:
+                    stage(pair)
+                else:
+                    stage(pair, which)
 
         for c in range(FIRST_LOADS):
             load_chunk(c)
-        for first in range(0, MEAN_TILES, 2):
-            bank = transpose_two(mean_words, first)
-            nc.scalar.copy(
-                out=mean_slots[:, first : first + 2],
-                in_=bank[:].rearrange("p a u (b k m) -> p a b k m u", k=OUTER, m=SEGMENTS),
-            )
+        def turn_means():
+            for first in range(0, MEAN_TILES, 2):
+                bank = transpose_two(mean_words, first, "se_again", 2)
+                nc.scalar.copy(
+                    out=mean_slots[:, first : first + 2],
+                    in_=bank[:].rearrange("p a u (b k m) -> p a b k m u", k=OUTER, m=SEGMENTS),
+                )
+
+        def rows_step(c):
+            return max(c + ROWS_LAG, MEANS_STEP + 1 + c // 2)
 
         for step in range(LAST_STEP + 1):
+            short = due(vector_stages, step)
+            if step == MEANS_LOAD_STEP:
+                for half in (slice(0, MEAN_TILES // 2), slice(MEAN_TILES // 2, MEAN_TILES)):
+                    nc.sync.dma_start(out=mean_raw[:, half, :], in_=mean_rows[:, half, :])
             if step % INNER == 0:
-                at(load_yn, step // INNER, OCTETS)
+                at(load_yn, step // INNER - YN_LOAD_STEP // INNER, OCTETS)
             at(load_chunk, step + FIRST_LOADS, CHUNKS)
-            at(square_rows, step - SQUARE_LAG, CHUNKS)
+            for k in range(OUTER):
+                for quadrant in range(4):
+                    if step == quadrant_step(k, quadrant):
+                        copy_quadrant(k, quadrant)
+            for c in range(CHUNKS):
+                if step == rows_step(c) + 1:
+                    square_rows(c)
             at_expert(find_norm_factor, step, FACTOR_LAG)
             at(regroup, step, CHUNKS)
-            if step == 0:
+            if step == MEANS_STEP - 1:
+                turn_means()
+            if step == MEANS_STEP:
                 quantise_means()
-            at(multiply_rows, step - ROWS_LAG, CHUNKS)
-            at(multiply_transposed, step - COLUMNS_LAG, CHUNKS)
-            at_expert(multiply_slots_and_tokens, step, LOGITS_LAG)
-            at_expert(spread_norm_factor, step, SPREAD_LAG)
+            run(short[0:1])
+            for c in range(CHUNKS):
+                if step == rows_step(c):
+                    multiply_rows(c)
+            at(multiply_again, step - AGAIN_LAG, CHUNKS)
+            at(turn_slots, step - TURN_LAG, CHUNKS)
+            for k in range(OUTER):
+                if step == logits_step(k):
+                    multiply_slots_and_tokens(k)
             at(quantise_chunk, step - QUANTISE_LAG, CHUNKS)
-            at_expert(copy_spread, step, SPREAD_LAG + 1)
-            at(normalise, step - NORMALISE_LAG, CHUNKS)
+            run(short[1:2])
+            at(normalise, step - SCALE_LAG, CHUNKS)
+            if (step - GROUP_LAG) % 2 == 1:
+                at(group_slots, (step - GROUP_LAG) // 2, CHUNKS // 2)
+            run(short[2:3])
             at(copy_yn, step - 1 - YN_FIRST_STEP, YN_BANKS)
             at(transpose_yn, step - YN_FIRST_STEP, YN_BANKS)
             at(quantise_yn, step - YN_QUANTISE_STEP, OUTER)
             at_expert(quantise_slots, step, SLOTS_LAG)
-            for quadrant in range(4):
-                at_expert(lambda k: copy_quadrant(k, quadrant), step, LOGITS_LAG + 1 + quadrant)
-            at_half(keep_own_group, step, OWN_GROUP_LAG)
-            at_half(exponentiate, step, OWN_GROUP_LAG + 1)
-            at_half(finish_disp, step, OWN_GROUP_LAG + 2)
-
-        def transpose_octets(source):
-            bank = psum.tile([P, OCTETS, P], FP32, tag="bank")
-            for i in range(OCTETS):
-                nc.tensor.transpose(bank[:, i, :], source[:, i].rearrange("p k s -> p (k s)"), ident[:])
-            return bank
-
-        logits_bank = transpose_octets(logits_t)
-        comb_powers = softmax_start(logits_bank[:].rearrange("p i (g q) -> p i g q", q=SLOTS), [OCTETS, OCTET])
-        nc.scalar.activation(out=comb_powers[:], in_=comb_powers[:], func=ACT.Exp)
-
-        disp_bank = transpose_octets(disp_t)
-        disp = work.tile([P, GROUPS, SLOTS], FP32, bufs=1)
-        nc.scalar.copy(out=disp[:], in_=disp_bank[:].rearrange("p i (g q) -> p (i g) q", q=SLOTS))
-        nc.sync.dma_start(out=out_0.rearrange("b g k s q -> (k s) (b g) q"), in_=disp[:])
-
-        comb = work.tile([P, OCTETS, OCTET, SLOTS], FP32, bufs=1)
-        softmax_end(comb_powers, comb[:], [OCTETS, OCTET])
-        nc.sync.dma_start(
-            out=out_1.rearrange("b g k s q -> (k s) (b g) q"), in_=comb[:].rearrange("p i g q -> p (i g) q")
-        )
+            run(short[3:])
+            run(due(other_stages, step))

@@ -34,7 +34,8 @@ VECTOR_COLUMNS = 384
 EARLY_VECTOR_COLUMNS = 336
 LATE_VECTOR_COLUMNS = 320
 LATE_STEPS = 6
-QUADRANT_LAG = 1
+QUADRANT_LAG = 2
+LOGITS_SLACK = 2
 
 FIRST_LOADS = 2
 W_BUFFERS = 8
@@ -359,7 +360,9 @@ def tile_hierarchicalsoftmoe2dblock_pb_kernel(tc, yn, means, w_slot2, out_0, out
                 at(stage, k, OUTER)
 
         def logits_step(k):
-            return max(INNER * k + SLOTS_LAG, YN_QUANTISE_STEP + k) + 1
+            slack = LOGITS_SLACK if k < OUTER - 1 else 0
+            ready = max(INNER * k + SLOTS_LAG + slack, YN_QUANTISE_STEP + k) + 1
+            return ready if k == 0 else max(ready, logits_step(k - 1) + QUADRANT_LAG + 1)
 
         def quadrant_step(k, quadrant):
             return logits_step(k) + (QUADRANT_LAG if k < OUTER - 1 else 1)
@@ -420,7 +423,7 @@ def tile_hierarchicalsoftmoe2dblock_pb_kernel(tc, yn, means, w_slot2, out_0, out
         def rows_step(c):
             return max(c + ROWS_LAG, MEANS_STEP + 1 + c // 2)
 
-        for step in range(LAST_STEP + 1):
+        for step in range(pair_step(PAIRS - 1) + 6):
             short = due(vector_stages, step)
             if step == MEANS_LOAD_STEP:
                 for half in (slice(0, MEAN_TILES // 2), slice(MEAN_TILES // 2, MEAN_TILES)):
@@ -428,10 +431,9 @@ def tile_hierarchicalsoftmoe2dblock_pb_kernel(tc, yn, means, w_slot2, out_0, out
             if step % INNER == 0:
                 at(load_yn, step // INNER - YN_LOAD_STEP // INNER, OCTETS)
             at(load_chunk, step + FIRST_LOADS, CHUNKS)
-            for k in range(OUTER):
-                for quadrant in range(4):
-                    if step == quadrant_step(k, quadrant):
-                        copy_quadrant(k, quadrant)
+            for quadrant in range(4):
+                if step == quadrant_step(OUTER - 1, quadrant):
+                    copy_quadrant(OUTER - 1, quadrant)
             for c in range(CHUNKS):
                 if step == rows_step(c) + 1:
                     square_rows(c)
@@ -461,4 +463,8 @@ def tile_hierarchicalsoftmoe2dblock_pb_kernel(tc, yn, means, w_slot2, out_0, out
             at(quantise_yn, step - YN_QUANTISE_STEP, OUTER)
             at_expert(quantise_slots, step, SLOTS_LAG)
             run(short[3:])
+            for k in range(OUTER - 1):
+                for quadrant in range(4):
+                    if step == quadrant_step(k, quadrant):
+                        copy_quadrant(k, quadrant)
             run(due(other_stages, step))

@@ -125,7 +125,7 @@ def tile_hierarchicalsoftmoe2dblock_pb_kernel(tc, yn, means, w_slot2, out_0, out
             )
 
         yn_rows = yn.flatten_outer_dims().rearrange("(g p) d -> p g d", p=P)
-        yn_words = yn_raw[:].bitcast(FP32).rearrange("p g (w u) -> p g u w", u=2)
+        yn_words = yn_raw[:].bitcast(FP32).rearrange("p g (u w) -> p g u w", u=2)
         yn_slots = yn_grouped[:].bitcast(FP32).rearrange("p k g s u -> p g k s u")
 
         def load_yn(i):
@@ -214,7 +214,7 @@ def tile_hierarchicalsoftmoe2dblock_pb_kernel(tc, yn, means, w_slot2, out_0, out
         def turn_slots(c):
             if c % 2 == 0:
                 slots_bank[c // 2] = psum.tile([P, 2, 2, P], FP32, name="slots_bank")
-            words = se2_rows[c][:].bitcast(FP32).rearrange("p (w u) -> p u w", u=2)
+            words = se2_rows[c][:].bitcast(FP32).rearrange("p (u w) -> p u w", u=2)
             for u in range(2):
                 nc.tensor.transpose(slots_bank[c // 2][:, c % 2, u, :], words[:, u, :], ident[:])
 

@@ -30,31 +30,19 @@ CHUNKS = OUTER * INNER
 MEAN_TILES = GROUPS * OUTER * SEGMENTS // P
 YN_BANKS = GROUPS // 2
 
-VECTOR_COLUMNS = 384
+VECTOR_COLUMNS = 464
 EARLY_VECTOR_COLUMNS = 336
-LATE_VECTOR_COLUMNS = 320
-LATE_STEPS = 6
-QUADRANT_LAG = 2
-LOGITS_SLACK = 2
+EARLY_STEPS = 4
 
-FIRST_LOADS = 2
+FIRST_LOADS = 3
 W_BUFFERS = 8
-QUANTISE_LAG = 1
-MEANS_STEP = 2
+MEANS_STEP = 3
 ROWS_LAG = 2
-SQUARE_LAG = ROWS_LAG + 1
-AGAIN_LAG = ROWS_LAG + 6
-SCALE_LAG = AGAIN_LAG + 1
-TURN_LAG = SCALE_LAG + 1
-GROUP_LAG = TURN_LAG + 1
-MEANS_LOAD_STEP = 0
-FACTOR_LAG = INNER - 1 + SQUARE_LAG
-SLOTS_LAG = INNER + GROUP_LAG
-PAIRS = OUTER // 2
-YN_LOAD_STEP = 4
-YN_FIRST_STEP = 6
+YN_LOAD_STEP = 3
+YN_FIRST_STEP = 5
 YN_QUANTISE_STEP = YN_FIRST_STEP + YN_BANKS + 1
-LAST_STEP = INNER * (OUTER - 1) + SLOTS_LAG + 3 + 5
+PAIRS = OUTER // 2
+FIRST_PAIRS = PAIRS - 2
 
 FLOPS = 2 * OUTER * ROWS * D * INNER * D + 2 * GROUPS * OUTER * TOKENS * SLOTS * D
 
@@ -66,7 +54,7 @@ def tile_hierarchicalsoftmoe2dblock_pb_kernel(tc, yn, means, w_slot2, out_0, out
         keep = ctx.enter_context(tc.tile_pool(name="keep", bufs=1))
         w_pool = ctx.enter_context(tc.tile_pool(name="w_pool", bufs=W_BUFFERS))
         grouped_pool = ctx.enter_context(tc.tile_pool(name="grouped_pool", bufs=3))
-        codes_pool = ctx.enter_context(tc.tile_pool(name="codes_pool", bufs=AGAIN_LAG + 1))
+        codes_pool = ctx.enter_context(tc.tile_pool(name="codes_pool", bufs=5))
         work = ctx.enter_context(tc.tile_pool(name="work", bufs=2))
         small = ctx.enter_context(tc.tile_pool(name="small", bufs=6))
         psum = ctx.enter_context(tc.psum_pool(name="psum", bufs=2))
@@ -80,10 +68,8 @@ def tile_hierarchicalsoftmoe2dblock_pb_kernel(tc, yn, means, w_slot2, out_0, out
             axis=AXIS.XY,
             op=ALU.add,
         )
-        minus_half = keep.tile([P, INNER], FP32)
-        nc.vector.memset(minus_half[:], -0.5)
         warm = keep.tile([P, 1], FP32)
-        nc.scalar.activation(out=warm[:], in_=minus_half[:, 0:1], func=ACT.Exp)
+        nc.scalar.activation(out=warm[:], in_=ident[:, 0:1], func=ACT.Abs_reciprocal_sqrt, scale=1.0, bias=1.0)
 
         mean_raw = keep.tile([P, MEAN_TILES, D], BF16)
         mean_grouped = keep.tile([P, OUTER, ROWS, PACK], BF16, align_bytes=64)
@@ -98,11 +84,14 @@ def tile_hierarchicalsoftmoe2dblock_pb_kernel(tc, yn, means, w_slot2, out_0, out
         two_groups = keep.tile([P, PAIRS, OCTETS, 2, 2, TOKENS], FP32)
         logits_t = keep.tile([P, PAIRS, OCTETS, 2, TOKENS], FP32)
         disp_t = keep.tile([P, PAIRS, OCTETS, 2, TOKENS], FP32)
+        disp_powers = keep.tile([P, PAIRS, OCTETS * 2, TOKENS], FP32)
+        comb_powers = keep.tile([P, PAIRS, OCTET, SLOTS], FP32)
+        disp_result = keep.tile([P, PAIRS, OCTET, SLOTS], FP32)
+        comb_result = keep.tile([P, PAIRS, OCTET, SLOTS], FP32)
 
         w_raw, grouped, w_codes, w_scales = {}, {}, {}, {}
-        se_rows, sum_squares, norm_factor, spread_bank, spread = {}, {}, {}, {}, {}
-        se_again, se2_rows, slots_bank, se2_grouped, yn_bank, all_pairs = {}, {}, {}, {}, {}, {}
-        even_part, top, powers, total, bank_of, result = {}, {}, {}, {}, {}, {}
+        se_rows, norm_factor, se2_rows, slots_bank, se2_grouped = {}, {}, {}, {}, {}
+        yn_bank, all_pairs, even_part, turned_logits, total = {}, {}, {}, {}, {}
 
         def transpose_two(words, first, tag, bufs):
             bank = psum.tile([P, 2, 2, P], FP32, tag=tag, bufs=bufs)
@@ -133,7 +122,7 @@ def tile_hierarchicalsoftmoe2dblock_pb_kernel(tc, yn, means, w_slot2, out_0, out
             nc.sync.dma_start(out=yn_raw[:, some, :], in_=yn_rows[:, some, :])
 
         def transpose_yn(b):
-            yn_bank[b] = transpose_two(yn_words, 2 * b, "turned", 1)
+            yn_bank[b] = transpose_two(yn_words, 2 * b, "turned", 3)
 
         def copy_yn(b):
             copy = nc.scalar.copy if b % 2 == 0 else nc.vector.tensor_copy
@@ -159,7 +148,7 @@ def tile_hierarchicalsoftmoe2dblock_pb_kernel(tc, yn, means, w_slot2, out_0, out
             grouped[c] = grouped_pool.tile([P, D, PACK], BF16, name="grouped", align_bytes=64)
             to_words = grouped[c][:].rearrange("p (n i) j -> p n j i", i=4)
             from_rows = w_raw[c][:].rearrange("p j (n i) -> p n j i", i=4)
-            fours = (EARLY_VECTOR_COLUMNS if c < SCALE_LAG else LATE_VECTOR_COLUMNS if c >= CHUNKS - LATE_STEPS else VECTOR_COLUMNS) // 4
+            fours = (EARLY_VECTOR_COLUMNS if c < EARLY_STEPS else VECTOR_COLUMNS) // 4
             nc.vector.tensor_copy(out=to_words[:, :fours], in_=from_rows[:, :fours])
             if fours < D // 4:
                 nc.scalar.copy(out=to_words[:, fours:], in_=from_rows[:, fours:])
@@ -174,7 +163,7 @@ def tile_hierarchicalsoftmoe2dblock_pb_kernel(tc, yn, means, w_slot2, out_0, out
             )
 
         def multiply_rows(c):
-            se_rows[c] = psum.tile([P, D], FP32, name="se_rows")
+            se_rows[c] = psum.tile([P, D], FP32, name="se_rows", bufs=3)
             nc.tensor.matmul_mx(
                 out=se_rows[c][:],
                 lhsT=mean_codes[:, c // INNER, :].bitcast(FP8X4),
@@ -186,30 +175,22 @@ def tile_hierarchicalsoftmoe2dblock_pb_kernel(tc, yn, means, w_slot2, out_0, out
             )
 
         def square_rows(c):
-            k, e = divmod(c, INNER)
-            if e == 0:
-                sum_squares[k] = small.tile([P, INNER], FP32, name="sum_squares")
+            norm_factor[c] = small.tile([P, 1], FP32, name="norm_factor")
             squares = work.tile([P, D], BF16)
-            nc.scalar.activation(
-                out=squares[:], in_=se_rows[c][:], func=ACT.Square, accum_out=sum_squares[k][:, e : e + 1]
-            )
+            nc.scalar.activation(out=squares[:], in_=se_rows[c][:], func=ACT.Square, accum_out=norm_factor[c][:])
 
-        def multiply_again(c):
-            se_again[c] = psum.tile([P, D], FP32, name="se_again")
-            nc.tensor.matmul_mx(
-                out=se_again[c][:],
-                lhsT=mean_codes[:, c // INNER, :].bitcast(FP8X4),
-                lhsT_scale=mean_scales[:, c // INNER, :],
-                rhs=w_codes[c][:].bitcast(FP8X4),
-                rhs_scale=w_scales[c][:],
-                start=True,
-                stop=True,
+        def find_norm_factor(c):
+            nc.scalar.activation(
+                out=norm_factor[c][:],
+                in_=norm_factor[c][:],
+                func=ACT.Abs_reciprocal_sqrt,
+                scale=1.0 / D,
+                bias=EPS / D,
             )
 
         def normalise(c):
-            k, e = divmod(c, INNER)
             se2_rows[c] = work.tile([P, D], BF16, name="se2_rows", bufs=3)
-            nc.scalar.activation(out=se2_rows[c][:], in_=se_again[c][:], func=ACT.Copy, scale=norm_factor[k][:, e : e + 1])
+            nc.scalar.activation(out=se2_rows[c][:], in_=se_rows[c][:], func=ACT.Copy, scale=norm_factor[c][:])
 
         def turn_slots(c):
             if c % 2 == 0:
@@ -224,19 +205,11 @@ def tile_hierarchicalsoftmoe2dblock_pb_kernel(tc, yn, means, w_slot2, out_0, out
                 se2_grouped[k] = work.tile(
                     [P, GROUPS, INNER, SEGMENTS, PACK], BF16, name="se2_grouped", align_bytes=64
                 )
-            copy = nc.scalar.copy if two % 2 == 0 else nc.vector.tensor_copy
+            copy = nc.scalar.copy if two < CHUNKS // 2 - 1 else nc.vector.tensor_copy
             copy(
                 out=se2_grouped[k][:].bitcast(FP32)[:, :, first : first + 2, :, :],
                 in_=slots_bank[two][:].rearrange("p e u (g m) -> p g e m u", m=SEGMENTS),
             )
-
-        def find_norm_factor(k):
-            mean_square = small.tile([P, INNER], FP32)
-            nc.gpsimd.tensor_scalar(
-                out=mean_square[:], in0=sum_squares[k][:], scalar1=1.0 / D, scalar2=EPS / D, op0=ALU.mult, op1=ALU.add
-            )
-            norm_factor[k] = small.tile([P, INNER], FP32, name="norm_factor")
-            nc.gpsimd.tensor_tensor(out=norm_factor[k][:], in0=mean_square[:], in1=minus_half[:], op=ALU.pow)
 
         def quantise_slots(k):
             nc.vector.quantize_mx(
@@ -246,7 +219,7 @@ def tile_hierarchicalsoftmoe2dblock_pb_kernel(tc, yn, means, w_slot2, out_0, out
             )
 
         def multiply_slots_and_tokens(k):
-            all_pairs[k] = psum.tile([P, OCTETS, P], FP32, name="all_pairs", bufs=1)
+            all_pairs[k] = psum.tile([P, OCTETS, P], FP32, tag="turned", name="all_pairs", bufs=3)
             for i in range(OCTETS):
                 block = slice(i * P, (i + 1) * P)
                 nc.tensor.matmul_mx(
@@ -259,26 +232,15 @@ def tile_hierarchicalsoftmoe2dblock_pb_kernel(tc, yn, means, w_slot2, out_0, out
                     stop=True,
                 )
 
-        def copy_quadrant(k, quadrant):
-            rows = slice(32 * quadrant, 32 * quadrant + 32)
-            nc.scalar.copy(
-                out=two_groups[rows, k // 2, :, k % 2],
-                in_=all_pairs[k][rows, :, 32 * quadrant : 32 * quadrant + 32].rearrange(
-                    "p i (h s) -> p i h s", h=2
-                ),
-            )
-
-        DISP, COMB = 0, 1
-        SETS = {DISP: [OCTETS, 2], COMB: [OCTET]}
-
-        def spread_last(values, which):
-            sets = SETS[which]
-            return values[:].unsqueeze(len(sets) + 1).to_broadcast([P] + sets + [TOKENS])
-
-        def logits_of(pair, which):
-            if which == DISP:
-                return logits_t[:, pair]
-            return bank_of[pair, COMB][:].rearrange("p (g q) -> p g q", q=SLOTS)
+        def copy_quadrants(k):
+            for quadrant in range(4):
+                rows = slice(32 * quadrant, 32 * quadrant + 32)
+                nc.scalar.copy(
+                    out=two_groups[rows, k // 2, :, k % 2],
+                    in_=all_pairs[k][rows, :, 32 * quadrant : 32 * quadrant + 32].rearrange(
+                        "p i (h s) -> p i h s", h=2
+                    ),
+                )
 
         def take_even_group(pair):
             even_part[pair] = work.tile([P, OCTETS, 2, TOKENS], FP32, name="even_part")
@@ -300,171 +262,217 @@ def tile_hierarchicalsoftmoe2dblock_pb_kernel(tc, yn, means, w_slot2, out_0, out
                 op1=ALU.add,
             )
 
+        def turn_logits(pair):
+            turned_logits[pair] = psum.tile([P, OCTET, SLOTS], FP32, tag="turned", name="turned_logits", bufs=3)
+            nc.tensor.transpose(
+                turned_logits[pair][:].rearrange("p g q -> p (g q)"),
+                logits_t[:, pair].rearrange("p i k s -> p (i k s)"),
+                ident[:],
+            )
+
+        def logits_of(pair, which):
+            return turned_logits[pair][:] if which == COMB else logits_t[:, pair].rearrange("p i k s -> p (i k) s")
+
         def find_top(pair, which):
-            top[pair, which] = small.tile([P] + SETS[which], FP32, name="top")
-            nc.vector.tensor_reduce(out=top[pair, which][:], in_=logits_of(pair, which), axis=AXIS.X, op=ALU.max)
+            total[pair, which] = small.tile([P, 8], FP32, name="total")
+            nc.vector.tensor_reduce(out=total[pair, which][:], in_=logits_of(pair, which), axis=AXIS.X, op=ALU.max)
 
         def subtract_top(pair, which):
-            powers[pair, which] = work.tile([P] + SETS[which] + [TOKENS], FP32, name="powers", bufs=4)
             nc.vector.tensor_tensor(
-                out=powers[pair, which][:],
+                out=POWERS[which][:, pair],
                 in0=logits_of(pair, which),
-                in1=spread_last(top[pair, which], which),
+                in1=total[pair, which][:].unsqueeze(2).to_broadcast([P, 8, 16]),
                 op=ALU.subtract,
             )
 
-        def exponentiate(pair, which):
-            nc.scalar.activation(out=powers[pair, which][:], in_=powers[pair, which][:], func=ACT.Exp)
+        DISP, COMB = 0, 1
+        POWERS = {DISP: disp_powers, COMB: comb_powers}
 
-        def find_total(pair, which):
-            total[pair, which] = small.tile([P] + SETS[which], FP32, name="total")
-            nc.vector.tensor_reduce(out=total[pair, which][:], in_=powers[pair, which][:], axis=AXIS.X, op=ALU.add)
+        def exponentiate(pairs, which):
+            nc.scalar.activation(out=POWERS[which][:, pairs], in_=POWERS[which][:, pairs], func=ACT.Exp)
 
-        def invert_total(pair, which):
-            nc.vector.reciprocal(out=total[pair, which][:], in_=total[pair, which][:])
+        def find_total(pairs, which):
+            total[pairs.start, which] = small.tile([P, PAIRS, 8], FP32, name="totals")
+            nc.vector.tensor_reduce(
+                out=total[pairs.start, which][:, pairs], in_=POWERS[which][:, pairs], axis=AXIS.X, op=ALU.add
+            )
 
-        def divide(pair, which):
-            if which == COMB:
-                result[pair, COMB] = work.tile([P, OCTET, SLOTS], FP32, name="comb")
+        def invert_total(pairs, which):
+            some = total[pairs.start, which][:, pairs]
+            nc.vector.reciprocal(out=some, in_=some)
+
+        def divide(pairs, which):
+            count = pairs.stop - pairs.start
+            out = comb_result[:, pairs] if which == COMB else disp_t[:, pairs].rearrange("p a i k s -> p a (i k) s")
             nc.vector.tensor_tensor(
-                out=disp_t[:, pair] if which == DISP else result[pair, COMB][:],
-                in0=powers[pair, which][:],
-                in1=spread_last(total[pair, which], which),
+                out=out,
+                in0=POWERS[which][:, pairs],
+                in1=total[pairs.start, which][:, pairs].unsqueeze(3).to_broadcast([P, count, 8, 16]),
                 op=ALU.mult,
             )
 
-        def transpose_pair(pair, which):
-            source = logits_t if which == COMB else disp_t
-            bank_of[pair, which] = psum.tile([P, P], FP32, tag="turned", name="bank_of", bufs=1)
-            nc.tensor.transpose(bank_of[pair, which][:], source[:, pair].rearrange("p i k s -> p (i k s)"), ident[:])
+        def turn_disp(pairs):
+            count = pairs.stop - pairs.start
+            bank = psum.tile([P, count, P], FP32, tag="turned", name="turned_disp", bufs=3)
+            for a in range(count):
+                nc.tensor.transpose(bank[:, a, :], disp_t[:, pairs.start + a].rearrange("p i k s -> p (i k s)"), ident[:])
+            nc.scalar.copy(
+                out=disp_result[:, pairs], in_=bank[:].rearrange("p a (g q) -> p a g q", q=SLOTS)
+            )
 
-        def copy_disp(pair):
-            result[pair, DISP] = work.tile([P, OCTET, SLOTS], FP32, name="disp")
-            nc.scalar.copy(out=result[pair, DISP][:], in_=bank_of[pair, DISP][:].rearrange("p (g q) -> p g q", q=SLOTS))
+        def store(pairs, which, queue):
+            out, result = (out_1, comb_result) if which == COMB else (out_0, disp_result)
+            for pair in range(pairs.start, pairs.stop):
+                for b in range(OCTETS):
+                    queue.dma_start(
+                        out=out[b, :, 2 * pair : 2 * pair + 2].rearrange("g k s q -> (k s) g q"),
+                        in_=result[32 * b : 32 * b + 32, pair],
+                    )
 
-        def store(pair, which):
-            out = out_0 if which == DISP else out_1
-            for b in range(OCTETS):
-                nc.sync.dma_start(
-                    out=out[b, :, 2 * pair : 2 * pair + 2].rearrange("g k s q -> (k s) g q"),
-                    in_=result[pair, which][32 * b : 32 * b + 32],
-                )
+        def rows_step(c):
+            return max(c + ROWS_LAG, MEANS_STEP + 1 + c // 2)
+
+        def normalise_step(c):
+            return rows_step(c) + 1
+
+        def turn_step(c):
+            return normalise_step(c) + 1
+
+        def group_step(two):
+            return turn_step(2 * two + 1) + 1
+
+        def slots_step(k):
+            return group_step(2 * k + 1) + 1
+
+        def tokens_step(k):
+            return YN_QUANTISE_STEP + (k // 2 if k < 2 * FIRST_PAIRS else 2 * k - 3 * FIRST_PAIRS)
+
+        def logits_step(k):
+            ready = max(slots_step(k), tokens_step(k)) + 1
+            return ready if k == 0 else max(ready, logits_step(k - 1) + 1)
+
+        def quadrant_step(k):
+            return logits_step(k) + 1
+
+        def pair_step(pair):
+            return quadrant_step(2 * pair + 1) + 1
 
         def at(stage, index, count):
             if 0 <= index < count:
                 stage(index)
 
-        def at_expert(stage, step, lag):
-            k, rest = divmod(step - lag, INNER)
-            if rest == 0:
-                at(stage, k, OUTER)
+        def due(stage, when, count, step):
+            for index in range(count):
+                if when(index) == step:
+                    stage(index)
 
-        def logits_step(k):
-            slack = LOGITS_SLACK if k < OUTER - 1 else 0
-            ready = max(INNER * k + SLOTS_LAG + slack, YN_QUANTISE_STEP + k) + 1
-            return ready if k == 0 else max(ready, logits_step(k - 1) + QUADRANT_LAG + 1)
-
-        def quadrant_step(k, quadrant):
-            return logits_step(k) + (QUADRANT_LAG if k < OUTER - 1 else 1)
-
-        def pair_step(pair):
-            ready = quadrant_step(2 * pair + 1, 3) + 1
-            return ready if pair == 0 else max(ready, pair_step(pair - 1) + 5)
-
-        vector_stages = [
-            (0, take_even_group, None),
-            (0, add_odd_group, None),
-            (0, find_top, DISP),
-            (1, subtract_top, DISP),
-            (2, find_top, COMB),
-            (2, subtract_top, COMB),
-            (3, find_total, DISP),
-            (3, invert_total, DISP),
-            (3, divide, DISP),
-            (4, find_total, COMB),
-            (4, invert_total, COMB),
-            (4, divide, COMB),
-        ]
-        other_stages = [
-            (1, transpose_pair, COMB),
-            (2, exponentiate, DISP),
-            (3, exponentiate, COMB),
-            (4, transpose_pair, DISP),
-            (5, copy_disp, None),
-            (5, store, DISP),
-            (5, store, COMB),
-        ]
-
-        def due(stages, step):
-            return [
-                (stage, pair, which)
-                for pair in range(PAIRS)
-                for lag, stage, which in stages
-                if step == pair_step(pair) + lag
-            ]
-
-        def run(some):
-            for stage, pair, which in some:
-                if which is None:
-                    stage(pair)
-                else:
-                    stage(pair, which)
-
-        for c in range(FIRST_LOADS):
-            load_chunk(c)
         def turn_means():
             for first in range(0, MEAN_TILES, 2):
-                bank = transpose_two(mean_words, first, "se_again", 2)
+                bank = transpose_two(mean_words, first, "se_rows", 3)
                 nc.scalar.copy(
                     out=mean_slots[:, first : first + 2],
                     in_=bank[:].rearrange("p a u (b k m) -> p a b k m u", k=OUTER, m=SEGMENTS),
                 )
 
-        def rows_step(c):
-            return max(c + ROWS_LAG, MEANS_STEP + 1 + c // 2)
+        def short_stages(step):
+            stages = []
+            for pair in range(PAIRS - 1):
+                since = step - pair_step(pair)
+                if since == 0:
+                    stages += [(take_even_group, pair), (add_odd_group, pair), (find_top, pair, DISP)]
+                elif since == 1:
+                    stages += [(subtract_top, pair, DISP)]
+                elif since == 2:
+                    stages += [(find_top, pair, COMB), (subtract_top, pair, COMB)]
+            if step == first_exponents + 1:
+                stages += [
+                    (find_total, first_pairs, DISP),
+                    (find_total, first_pairs, COMB),
+                    (invert_total, first_pairs, DISP),
+                    (invert_total, first_pairs, COMB),
+                    (divide, first_pairs, DISP),
+                    (divide, first_pairs, COMB),
+                ]
+            return stages
 
-        for step in range(pair_step(PAIRS - 1) + 6):
-            short = due(vector_stages, step)
-            if step == MEANS_LOAD_STEP:
-                for half in (slice(0, MEAN_TILES // 2), slice(MEAN_TILES // 2, MEAN_TILES)):
-                    nc.sync.dma_start(out=mean_raw[:, half, :], in_=mean_rows[:, half, :])
-            if step % INNER == 0:
-                at(load_yn, step // INNER - YN_LOAD_STEP // INNER, OCTETS)
+        def run(stages):
+            for stage in stages:
+                stage[0](*stage[1:])
+
+        for c in range(FIRST_LOADS):
+            load_chunk(c)
+        for half in (slice(0, MEAN_TILES // 2), slice(MEAN_TILES // 2, MEAN_TILES)):
+            nc.sync.dma_start(out=mean_raw[:, half, :], in_=mean_rows[:, half, :])
+
+        first_pairs = slice(0, FIRST_PAIRS)
+        next_pair = slice(FIRST_PAIRS, FIRST_PAIRS + 1)
+        last_pair = slice(FIRST_PAIRS + 1, PAIRS)
+        last = PAIRS - 1
+        first_exponents = pair_step(FIRST_PAIRS - 1) + 2
+
+        for step in range(quadrant_step(OUTER - 1)):
+            short = short_stages(step)
+            if (step - YN_LOAD_STEP) % INNER == 0:
+                at(load_yn, (step - YN_LOAD_STEP) // INNER, OCTETS)
             at(load_chunk, step + FIRST_LOADS, CHUNKS)
-            for quadrant in range(4):
-                if step == quadrant_step(OUTER - 1, quadrant):
-                    copy_quadrant(OUTER - 1, quadrant)
-            for c in range(CHUNKS):
-                if step == rows_step(c) + 1:
-                    square_rows(c)
-            at_expert(find_norm_factor, step, FACTOR_LAG)
+            due(square_rows, normalise_step, CHUNKS, step)
             at(regroup, step, CHUNKS)
+            due(find_norm_factor, normalise_step, CHUNKS, step)
             if step == MEANS_STEP - 1:
                 turn_means()
             if step == MEANS_STEP:
                 quantise_means()
             run(short[0:1])
-            for c in range(CHUNKS):
-                if step == rows_step(c):
-                    multiply_rows(c)
-            at(multiply_again, step - AGAIN_LAG, CHUNKS)
-            at(turn_slots, step - TURN_LAG, CHUNKS)
-            for k in range(OUTER):
-                if step == logits_step(k):
-                    multiply_slots_and_tokens(k)
-            at(quantise_chunk, step - QUANTISE_LAG, CHUNKS)
+            due(turn_slots, turn_step, CHUNKS, step)
+            at(quantise_chunk, step - 1, CHUNKS)
             run(short[1:2])
-            at(normalise, step - SCALE_LAG, CHUNKS)
-            if (step - GROUP_LAG) % 2 == 1:
-                at(group_slots, (step - GROUP_LAG) // 2, CHUNKS // 2)
-            run(short[2:3])
+            due(group_slots, group_step, CHUNKS // 2, step)
             at(copy_yn, step - 1 - YN_FIRST_STEP, YN_BANKS)
             at(transpose_yn, step - YN_FIRST_STEP, YN_BANKS)
-            at(quantise_yn, step - YN_QUANTISE_STEP, OUTER)
-            at_expert(quantise_slots, step, SLOTS_LAG)
-            run(short[3:])
-            for k in range(OUTER - 1):
-                for quadrant in range(4):
-                    if step == quadrant_step(k, quadrant):
-                        copy_quadrant(k, quadrant)
-            run(due(other_stages, step))
+            due(turn_logits, lambda pair: pair_step(pair) + 1, PAIRS - 1, step)
+            due(normalise, normalise_step, CHUNKS, step)
+            due(quantise_yn, tokens_step, OUTER, step)
+            due(quantise_slots, slots_step, OUTER, step)
+            run(short[2:])
+            due(copy_quadrants, quadrant_step, OUTER, step)
+            due(multiply_rows, rows_step, CHUNKS, step)
+            due(multiply_slots_and_tokens, logits_step, OUTER, step)
+            if step == first_exponents + 2:
+                turn_disp(first_pairs)
+                for which in (DISP, COMB):
+                    store(first_pairs, which, nc.sync)
+            if step == first_exponents:
+                exponentiate(first_pairs, DISP)
+                exponentiate(first_pairs, COMB)
+            if step == normalise_step(CHUNKS - 1) + 1:
+                exponentiate(next_pair, DISP)
+                exponentiate(next_pair, COMB)
+
+        find_total(next_pair, DISP)
+        find_total(next_pair, COMB)
+        copy_quadrants(OUTER - 1)
+        invert_total(next_pair, DISP)
+        invert_total(next_pair, COMB)
+        divide(next_pair, DISP)
+        divide(next_pair, COMB)
+        take_even_group(last)
+        add_odd_group(last)
+        turn_disp(next_pair)
+        turn_logits(last)
+        for which in (DISP, COMB):
+            store(next_pair, which, nc.sync)
+        find_top(last, DISP)
+        subtract_top(last, DISP)
+        exponentiate(last_pair, DISP)
+        find_top(last, COMB)
+        subtract_top(last, COMB)
+        exponentiate(last_pair, COMB)
+        find_total(last_pair, DISP)
+        invert_total(last_pair, DISP)
+        find_total(last_pair, COMB)
+        divide(last_pair, DISP)
+        turn_disp(last_pair)
+        invert_total(last_pair, COMB)
+        divide(last_pair, COMB)
+        store(last_pair, COMB, nc.sync)
+        store(last_pair, DISP, nc.scalar)

@@ -30,19 +30,30 @@ CHUNKS = OUTER * INNER
 MEAN_TILES = GROUPS * OUTER * SEGMENTS // P
 YN_BANKS = GROUPS // 2
 
-VECTOR_COLUMNS = 464
+VECTOR_COLUMNS = 448
 EARLY_VECTOR_COLUMNS = 336
 EARLY_STEPS = 4
+VECTOR_GROUPS = 3
+LATE_STEPS = 2
 
-FIRST_LOADS = 3
-W_BUFFERS = 8
-MEANS_STEP = 3
-ROWS_LAG = 2
-YN_LOAD_STEP = 3
-YN_FIRST_STEP = 5
+SINGLE_LOADS = 4
+FIRST_LOADS = 2
+PAIR_BUFFERS = 4
+MEANS_STEP = 2
+CODES_BUFFERS = 8
+QUANTISE_LAG = 1
+ROWS_LAG = QUANTISE_LAG + 1
+NORMALISE_LAG = 1
+TURN_LAG = 1
+GROUP_LAG = 1
+YN_LOAD_STEP = 5
+YN_LOAD_EVERY = 4
+YN_FIRST_STEP = 7
 YN_QUANTISE_STEP = YN_FIRST_STEP + YN_BANKS + 1
 PAIRS = OUTER // 2
 FIRST_PAIRS = PAIRS - 2
+
+TURN_STRIDE = P + SLOTS
 
 FLOPS = 2 * OUTER * ROWS * D * INNER * D + 2 * GROUPS * OUTER * TOKENS * SLOTS * D
 
@@ -52,22 +63,15 @@ def tile_hierarchicalsoftmoe2dblock_pb_kernel(tc, yn, means, w_slot2, out_0, out
     with ExitStack() as ctx:
         ctx.enter_context(tc.manual_schedule())
         keep = ctx.enter_context(tc.tile_pool(name="keep", bufs=1))
-        w_pool = ctx.enter_context(tc.tile_pool(name="w_pool", bufs=W_BUFFERS))
-        grouped_pool = ctx.enter_context(tc.tile_pool(name="grouped_pool", bufs=3))
-        codes_pool = ctx.enter_context(tc.tile_pool(name="codes_pool", bufs=5))
+        w_pool = ctx.enter_context(tc.tile_pool(name="w_pool", bufs=PAIR_BUFFERS))
+        grouped_pool = ctx.enter_context(tc.tile_pool(name="grouped_pool", bufs=QUANTISE_LAG + 2))
+        codes_pool = ctx.enter_context(tc.tile_pool(name="codes_pool", bufs=CODES_BUFFERS))
         work = ctx.enter_context(tc.tile_pool(name="work", bufs=2))
         small = ctx.enter_context(tc.tile_pool(name="small", bufs=6))
         psum = ctx.enter_context(tc.psum_pool(name="psum", bufs=2))
 
         ident = keep.tile([P, P], FP32)
         make_identity(nc, ident[:])
-        parity = keep.tile([P, 2], FP32)
-        nc.vector.tensor_reduce(
-            out=parity[:],
-            in_=ident[:].rearrange("p (q h c) -> p h q c", h=2, c=TOKENS),
-            axis=AXIS.XY,
-            op=ALU.add,
-        )
         warm = keep.tile([P, 1], FP32)
         nc.scalar.activation(out=warm[:], in_=ident[:, 0:1], func=ACT.Abs_reciprocal_sqrt, scale=1.0, bias=1.0)
 
@@ -75,23 +79,20 @@ def tile_hierarchicalsoftmoe2dblock_pb_kernel(tc, yn, means, w_slot2, out_0, out
         mean_grouped = keep.tile([P, OUTER, ROWS, PACK], BF16, align_bytes=64)
         mean_codes = keep.tile([P, OUTER, ROWS], U32, align_bytes=64)
         mean_scales = keep.tile([P, OUTER, ROWS], U8, align_bytes=64)
-        yn_raw = keep.tile([P, GROUPS, D], BF16)
         yn_grouped = keep.tile([P, OUTER, GROUPS, TOKENS, PACK], BF16, align_bytes=64)
         yn_codes = keep.tile([P, OUTER, GROUPS * TOKENS], U32, align_bytes=64)
         yn_scales = keep.tile([P, OUTER, GROUPS * TOKENS], U8, align_bytes=64)
         se2_codes = keep.tile([P, OUTER, GROUPS * SLOTS], U32, align_bytes=64)
         se2_scales = keep.tile([P, OUTER, GROUPS * SLOTS], U8, align_bytes=64)
-        two_groups = keep.tile([P, PAIRS, OCTETS, 2, 2, TOKENS], FP32)
-        logits_t = keep.tile([P, PAIRS, OCTETS, 2, TOKENS], FP32)
-        disp_t = keep.tile([P, PAIRS, OCTETS, 2, TOKENS], FP32)
-        disp_powers = keep.tile([P, PAIRS, OCTETS * 2, TOKENS], FP32)
+        two_groups = keep.tile([P, PAIRS, 2, OCTETS, 2, TOKENS], FP32)
+        disp_powers = keep.tile([P, PAIRS, 2 * OCTETS * 2, TOKENS], FP32)
         comb_powers = keep.tile([P, PAIRS, OCTET, SLOTS], FP32)
         disp_result = keep.tile([P, PAIRS, OCTET, SLOTS], FP32)
         comb_result = keep.tile([P, PAIRS, OCTET, SLOTS], FP32)
 
-        w_raw, grouped, w_codes, w_scales = {}, {}, {}, {}
+        w_raw, yn_raw, grouped, w_codes, w_scales = {}, {}, {}, {}, {}
         se_rows, norm_factor, se2_rows, slots_bank, se2_grouped = {}, {}, {}, {}, {}
-        yn_bank, all_pairs, even_part, turned_logits, total = {}, {}, {}, {}, {}
+        yn_bank, all_pairs, turned_logits, total = {}, {}, {}, {}
 
         def transpose_two(words, first, tag, bufs):
             bank = psum.tile([P, 2, 2, P], FP32, tag=tag, bufs=bufs)
@@ -114,15 +115,17 @@ def tile_hierarchicalsoftmoe2dblock_pb_kernel(tc, yn, means, w_slot2, out_0, out
             )
 
         yn_rows = yn.flatten_outer_dims().rearrange("(g p) d -> p g d", p=P)
-        yn_words = yn_raw[:].bitcast(FP32).rearrange("p g (u w) -> p g u w", u=2)
         yn_slots = yn_grouped[:].bitcast(FP32).rearrange("p k g s u -> p g k s u")
 
         def load_yn(i):
             some = slice(i * OCTET, (i + 1) * OCTET)
-            nc.sync.dma_start(out=yn_raw[:, some, :], in_=yn_rows[:, some, :])
+            yn_raw[i] = w_pool.tile([P, OCTET, D], BF16, name="yn_raw", bufs=2)
+            nc.sync.dma_start(out=yn_raw[i][:], in_=yn_rows[:, some, :])
 
         def transpose_yn(b):
-            yn_bank[b] = transpose_two(yn_words, 2 * b, "turned", 3)
+            i, first = divmod(2 * b, OCTET)
+            words = yn_raw[i][:].bitcast(FP32).rearrange("p g (u w) -> p g u w", u=2)
+            yn_bank[b] = transpose_two(words, first, "turned", 3)
 
         def copy_yn(b):
             copy = nc.scalar.copy if b % 2 == 0 else nc.vector.tensor_copy
@@ -138,19 +141,22 @@ def tile_hierarchicalsoftmoe2dblock_pb_kernel(tc, yn, means, w_slot2, out_0, out
                 in_=yn_grouped[:, k].rearrange("p g s t -> p (g s t)"),
             )
 
-        def load_chunk(c):
+        def load_chunks(c, count):
             k, e = divmod(c, INNER)
-            w_raw[c] = w_pool.tile([P, PACK, D], BF16, name="w_raw")
+            both = w_pool.tile([P, PACK, count * D], BF16, name="w_single" if count == 1 else "w_pair")
             rows = w_slot2[k].rearrange("(p j) n -> p j n", j=PACK)
-            nc.sync.dma_start(out=w_raw[c][:], in_=rows[:, :, e * D : (e + 1) * D])
+            nc.sync.dma_start(out=both[:], in_=rows[:, :, e * D : (e + count) * D])
+            for i in range(count):
+                w_raw[c + i] = both[:, :, i * D : (i + 1) * D]
 
         def regroup(c):
             grouped[c] = grouped_pool.tile([P, D, PACK], BF16, name="grouped", align_bytes=64)
             to_words = grouped[c][:].rearrange("p (n i) j -> p n j i", i=4)
-            from_rows = w_raw[c][:].rearrange("p j (n i) -> p n j i", i=4)
-            fours = (EARLY_VECTOR_COLUMNS if c < EARLY_STEPS else VECTOR_COLUMNS) // 4
+            from_rows = w_raw[c].rearrange("p j (n i) -> p n j i", i=4)
+            columns = EARLY_VECTOR_COLUMNS if c < EARLY_STEPS else VECTOR_COLUMNS if c < CHUNKS - LATE_STEPS else D
+            fours = columns // 4
             nc.vector.tensor_copy(out=to_words[:, :fours], in_=from_rows[:, :fours])
-            if fours < D // 4:
+            if columns < D:
                 nc.scalar.copy(out=to_words[:, fours:], in_=from_rows[:, fours:])
 
         def quantise_chunk(c):
@@ -205,7 +211,7 @@ def tile_hierarchicalsoftmoe2dblock_pb_kernel(tc, yn, means, w_slot2, out_0, out
                 se2_grouped[k] = work.tile(
                     [P, GROUPS, INNER, SEGMENTS, PACK], BF16, name="se2_grouped", align_bytes=64
                 )
-            copy = nc.scalar.copy if two < CHUNKS // 2 - 1 else nc.vector.tensor_copy
+            copy = nc.scalar.copy if two < CHUNKS // 2 - VECTOR_GROUPS else nc.vector.tensor_copy
             copy(
                 out=se2_grouped[k][:].bitcast(FP32)[:, :, first : first + 2, :, :],
                 in_=slots_bank[two][:].rearrange("p e u (g m) -> p g e m u", m=SEGMENTS),
@@ -236,63 +242,53 @@ def tile_hierarchicalsoftmoe2dblock_pb_kernel(tc, yn, means, w_slot2, out_0, out
             for quadrant in range(4):
                 rows = slice(32 * quadrant, 32 * quadrant + 32)
                 nc.scalar.copy(
-                    out=two_groups[rows, k // 2, :, k % 2],
+                    out=two_groups[rows, k // 2, :, :, k % 2],
                     in_=all_pairs[k][rows, :, 32 * quadrant : 32 * quadrant + 32].rearrange(
-                        "p i (h s) -> p i h s", h=2
+                        "p i (h s) -> p h i s", h=2
                     ),
                 )
 
-        def take_even_group(pair):
-            even_part[pair] = work.tile([P, OCTETS, 2, TOKENS], FP32, name="even_part")
-            nc.vector.tensor_scalar(
-                out=even_part[pair][:],
-                in0=two_groups[:, pair, :, :, 0, :],
-                scalar1=parity[:, 0:1],
-                scalar2=None,
-                op0=ALU.mult,
-            )
-
-        def add_odd_group(pair):
-            nc.vector.scalar_tensor_tensor(
-                out=logits_t[:, pair],
-                in0=two_groups[:, pair, :, :, 1, :],
-                scalar=parity[:, 1:2],
-                in1=even_part[pair][:],
-                op0=ALU.mult,
-                op1=ALU.add,
-            )
+        def turn(source, pair):
+            bank = psum.tile([P, 2 * TURN_STRIDE], FP32, tag="turned", name="bank", bufs=3)
+            for h in range(2):
+                nc.tensor.transpose(bank[:, h * P : (h + 1) * P], source[h], ident[:])
+            halves = bank[:].rearrange("p (h r) -> p h r", h=2)[:, :, 0:P]
+            return halves.rearrange("p h (a b q) -> p a h b q", b=2, q=SLOTS)[:, :, :, 0, :]
 
         def turn_logits(pair):
-            turned_logits[pair] = psum.tile([P, OCTET, SLOTS], FP32, tag="turned", name="turned_logits", bufs=3)
-            nc.tensor.transpose(
-                turned_logits[pair][:].rearrange("p g q -> p (g q)"),
-                logits_t[:, pair].rearrange("p i k s -> p (i k s)"),
-                ident[:],
+            turned_logits[pair] = turn(
+                [two_groups[:, pair, h].rearrange("p i k s -> p (i k s)") for h in range(2)], pair
             )
-
-        def logits_of(pair, which):
-            return turned_logits[pair][:] if which == COMB else logits_t[:, pair].rearrange("p i k s -> p (i k) s")
 
         def find_top(pair, which):
-            total[pair, which] = small.tile([P, 8], FP32, name="total")
-            nc.vector.tensor_reduce(out=total[pair, which][:], in_=logits_of(pair, which), axis=AXIS.X, op=ALU.max)
+            if which == COMB:
+                total[pair, COMB] = small.tile([P, OCTET // 2, 2], FP32, name="comb_top")
+                logits = turned_logits[pair]
+            else:
+                total[pair, DISP] = small.tile([P, 2 * OCTETS * 2], FP32, name="disp_top")
+                logits = two_groups[:, pair].rearrange("p h i k s -> p (h i k) s")
+            nc.vector.tensor_reduce(out=total[pair, which][:], in_=logits, axis=AXIS.X, op=ALU.max)
 
         def subtract_top(pair, which):
-            nc.vector.tensor_tensor(
-                out=POWERS[which][:, pair],
-                in0=logits_of(pair, which),
-                in1=total[pair, which][:].unsqueeze(2).to_broadcast([P, 8, 16]),
-                op=ALU.subtract,
-            )
+            if which == COMB:
+                out = comb_powers[:, pair].rearrange("p (a h) q -> p a h q", h=2)
+                logits = turned_logits[pair]
+                tops = total[pair, COMB][:].unsqueeze(3).to_broadcast([P, OCTET // 2, 2, SLOTS])
+            else:
+                out = disp_powers[:, pair]
+                logits = two_groups[:, pair].rearrange("p h i k s -> p (h i k) s")
+                tops = total[pair, DISP][:].unsqueeze(2).to_broadcast([P, 2 * OCTETS * 2, TOKENS])
+            nc.vector.tensor_tensor(out=out, in0=logits, in1=tops, op=ALU.subtract)
 
         DISP, COMB = 0, 1
         POWERS = {DISP: disp_powers, COMB: comb_powers}
+        SETS = {DISP: 2 * OCTETS * 2, COMB: OCTET}
 
         def exponentiate(pairs, which):
             nc.scalar.activation(out=POWERS[which][:, pairs], in_=POWERS[which][:, pairs], func=ACT.Exp)
 
         def find_total(pairs, which):
-            total[pairs.start, which] = small.tile([P, PAIRS, 8], FP32, name="totals")
+            total[pairs.start, which] = small.tile([P, PAIRS, SETS[which]], FP32, name="disp_total" if which == DISP else "comb_total")
             nc.vector.tensor_reduce(
                 out=total[pairs.start, which][:, pairs], in_=POWERS[which][:, pairs], axis=AXIS.X, op=ALU.add
             )
@@ -303,22 +299,20 @@ def tile_hierarchicalsoftmoe2dblock_pb_kernel(tc, yn, means, w_slot2, out_0, out
 
         def divide(pairs, which):
             count = pairs.stop - pairs.start
-            out = comb_result[:, pairs] if which == COMB else disp_t[:, pairs].rearrange("p a i k s -> p a (i k) s")
             nc.vector.tensor_tensor(
-                out=out,
+                out=comb_result[:, pairs] if which == COMB else disp_powers[:, pairs],
                 in0=POWERS[which][:, pairs],
-                in1=total[pairs.start, which][:, pairs].unsqueeze(3).to_broadcast([P, count, 8, 16]),
+                in1=total[pairs.start, which][:, pairs].unsqueeze(3).to_broadcast([P, count, SETS[which], 16]),
                 op=ALU.mult,
             )
 
         def turn_disp(pairs):
-            count = pairs.stop - pairs.start
-            bank = psum.tile([P, count, P], FP32, tag="turned", name="turned_disp", bufs=3)
-            for a in range(count):
-                nc.tensor.transpose(bank[:, a, :], disp_t[:, pairs.start + a].rearrange("p i k s -> p (i k s)"), ident[:])
-            nc.scalar.copy(
-                out=disp_result[:, pairs], in_=bank[:].rearrange("p a (g q) -> p a g q", q=SLOTS)
-            )
+            for pair in range(pairs.start, pairs.stop):
+                halves = disp_powers[:, pair].rearrange("p (h r) s -> p h (r s)", h=2)
+                nc.scalar.copy(
+                    out=disp_result[:, pair].rearrange("p (a h) q -> p a h q", h=2),
+                    in_=turn([halves[:, h] for h in range(2)], pair),
+                )
 
         def store(pairs, which, queue):
             out, result = (out_1, comb_result) if which == COMB else (out_0, disp_result)
@@ -332,14 +326,17 @@ def tile_hierarchicalsoftmoe2dblock_pb_kernel(tc, yn, means, w_slot2, out_0, out
         def rows_step(c):
             return max(c + ROWS_LAG, MEANS_STEP + 1 + c // 2)
 
-        def normalise_step(c):
+        def square_step(c):
             return rows_step(c) + 1
 
+        def normalise_step(c):
+            return square_step(c) + NORMALISE_LAG
+
         def turn_step(c):
-            return normalise_step(c) + 1
+            return normalise_step(c) + TURN_LAG
 
         def group_step(two):
-            return turn_step(2 * two + 1) + 1
+            return turn_step(2 * two + 1) + GROUP_LAG
 
         def slots_step(k):
             return group_step(2 * k + 1) + 1
@@ -379,11 +376,11 @@ def tile_hierarchicalsoftmoe2dblock_pb_kernel(tc, yn, means, w_slot2, out_0, out
             for pair in range(PAIRS - 1):
                 since = step - pair_step(pair)
                 if since == 0:
-                    stages += [(take_even_group, pair), (add_odd_group, pair), (find_top, pair, DISP)]
+                    stages += [(find_top, pair, DISP)]
                 elif since == 1:
-                    stages += [(subtract_top, pair, DISP)]
+                    stages += [(subtract_top, pair, DISP), (find_top, pair, COMB)]
                 elif since == 2:
-                    stages += [(find_top, pair, COMB), (subtract_top, pair, COMB)]
+                    stages += [(subtract_top, pair, COMB)]
             if step == first_exponents + 1:
                 stages += [
                     (find_total, first_pairs, DISP),
@@ -400,9 +397,11 @@ def tile_hierarchicalsoftmoe2dblock_pb_kernel(tc, yn, means, w_slot2, out_0, out
                 stage[0](*stage[1:])
 
         for c in range(FIRST_LOADS):
-            load_chunk(c)
+            load_chunks(c, 1)
         for half in (slice(0, MEAN_TILES // 2), slice(MEAN_TILES // 2, MEAN_TILES)):
             nc.sync.dma_start(out=mean_raw[:, half, :], in_=mean_rows[:, half, :])
+        for c in range(FIRST_LOADS, SINGLE_LOADS):
+            load_chunks(c, 1)
 
         first_pairs = slice(0, FIRST_PAIRS)
         next_pair = slice(FIRST_PAIRS, FIRST_PAIRS + 1)
@@ -412,31 +411,32 @@ def tile_hierarchicalsoftmoe2dblock_pb_kernel(tc, yn, means, w_slot2, out_0, out
 
         for step in range(quadrant_step(OUTER - 1)):
             short = short_stages(step)
-            if (step - YN_LOAD_STEP) % INNER == 0:
-                at(load_yn, (step - YN_LOAD_STEP) // INNER, OCTETS)
-            at(load_chunk, step + FIRST_LOADS, CHUNKS)
-            due(square_rows, normalise_step, CHUNKS, step)
+            if (step - YN_LOAD_STEP) % YN_LOAD_EVERY == 0:
+                at(load_yn, (step - YN_LOAD_STEP) // YN_LOAD_EVERY, OCTETS)
+            if step % 2 == 0 and SINGLE_LOADS + step < CHUNKS:
+                load_chunks(SINGLE_LOADS + step, 2)
+            due(square_rows, square_step, CHUNKS, step)
+            due(normalise, normalise_step, CHUNKS, step)
             at(regroup, step, CHUNKS)
-            due(find_norm_factor, normalise_step, CHUNKS, step)
+            due(find_norm_factor, square_step, CHUNKS, step)
             if step == MEANS_STEP - 1:
                 turn_means()
             if step == MEANS_STEP:
                 quantise_means()
             run(short[0:1])
-            due(turn_slots, turn_step, CHUNKS, step)
-            at(quantise_chunk, step - 1, CHUNKS)
-            run(short[1:2])
+            due(multiply_rows, rows_step, CHUNKS, step)
+            due(multiply_slots_and_tokens, logits_step, OUTER, step)
             due(group_slots, group_step, CHUNKS // 2, step)
             at(copy_yn, step - 1 - YN_FIRST_STEP, YN_BANKS)
             at(transpose_yn, step - YN_FIRST_STEP, YN_BANKS)
-            due(turn_logits, lambda pair: pair_step(pair) + 1, PAIRS - 1, step)
-            due(normalise, normalise_step, CHUNKS, step)
+            due(turn_slots, turn_step, CHUNKS, step)
+            due(turn_logits, pair_step, PAIRS - 1, step)
+            at(quantise_chunk, step - QUANTISE_LAG, CHUNKS)
+            run(short[1:2])
             due(quantise_yn, tokens_step, OUTER, step)
             due(quantise_slots, slots_step, OUTER, step)
             run(short[2:])
             due(copy_quadrants, quadrant_step, OUTER, step)
-            due(multiply_rows, rows_step, CHUNKS, step)
-            due(multiply_slots_and_tokens, logits_step, OUTER, step)
             if step == first_exponents + 2:
                 turn_disp(first_pairs)
                 for which in (DISP, COMB):
@@ -455,13 +455,11 @@ def tile_hierarchicalsoftmoe2dblock_pb_kernel(tc, yn, means, w_slot2, out_0, out
         invert_total(next_pair, COMB)
         divide(next_pair, DISP)
         divide(next_pair, COMB)
-        take_even_group(last)
-        add_odd_group(last)
-        turn_disp(next_pair)
         turn_logits(last)
+        find_top(last, DISP)
+        turn_disp(next_pair)
         for which in (DISP, COMB):
             store(next_pair, which, nc.sync)
-        find_top(last, DISP)
         subtract_top(last, DISP)
         exponentiate(last_pair, DISP)
         find_top(last, COMB)

@@ -30,30 +30,28 @@ CHUNKS = OUTER * INNER
 MEAN_TILES = GROUPS * OUTER * SEGMENTS // P
 YN_BANKS = GROUPS // 2
 
-VECTOR_COLUMNS = 448
-EARLY_VECTOR_COLUMNS = 336
-EARLY_STEPS = 4
-VECTOR_GROUPS = 3
-LATE_STEPS = 2
-
 SINGLE_LOADS = 4
-FIRST_LOADS = 2
 PAIR_BUFFERS = 4
 MEANS_STEP = 2
-CODES_BUFFERS = 8
+CODES_BUFFERS = 5
 QUANTISE_LAG = 1
 ROWS_LAG = QUANTISE_LAG + 1
 NORMALISE_LAG = 1
 TURN_LAG = 1
 GROUP_LAG = 1
-YN_LOAD_STEP = 5
+YN_LOAD_STEP = 8
 YN_LOAD_EVERY = 4
-YN_FIRST_STEP = 7
+LATE_TOKENS_FROM = 6
+A_DELAY = 2
+B_DELAY = 5
+LOGITS_LAG = 1
+LATE_LOGITS_LAG = 3
+YN_FIRST_STEP = 10
 YN_QUANTISE_STEP = YN_FIRST_STEP + YN_BANKS + 1
-PAIRS = OUTER // 2
-FIRST_PAIRS = PAIRS - 2
+BATCH = 4
 
 TURN_STRIDE = P + SLOTS
+TILES = OCTETS * BATCH * TOKENS // P
 
 FLOPS = 2 * OUTER * ROWS * D * INNER * D + 2 * GROUPS * OUTER * TOKENS * SLOTS * D
 
@@ -84,15 +82,17 @@ def tile_hierarchicalsoftmoe2dblock_pb_kernel(tc, yn, means, w_slot2, out_0, out
         yn_scales = keep.tile([P, OUTER, GROUPS * TOKENS], U8, align_bytes=64)
         se2_codes = keep.tile([P, OUTER, GROUPS * SLOTS], U32, align_bytes=64)
         se2_scales = keep.tile([P, OUTER, GROUPS * SLOTS], U8, align_bytes=64)
-        two_groups = keep.tile([P, PAIRS, 2, OCTETS, 2, TOKENS], FP32)
-        disp_powers = keep.tile([P, PAIRS, 2 * OCTETS * 2, TOKENS], FP32)
-        comb_powers = keep.tile([P, PAIRS, OCTET, SLOTS], FP32)
-        disp_result = keep.tile([P, PAIRS, OCTET, SLOTS], FP32)
-        comb_result = keep.tile([P, PAIRS, OCTET, SLOTS], FP32)
+        two_groups = keep.tile([P, OUTER // BATCH, 2, OCTETS, BATCH, TOKENS], FP32)
+        disp_powers = keep.tile([P, OUTER // BATCH, 2, OCTETS, BATCH, TOKENS], FP32)
+        disp_sums = keep.tile([P, OUTER // BATCH, 2, OCTETS, BATCH], FP32)
+        comb_powers = keep.tile([P, OUTER // BATCH, TILES, OCTET, SLOTS], FP32)
+        comb_sums = keep.tile([P, OUTER // BATCH, TILES, OCTET // 2, 2], FP32)
+        disp_result = keep.tile([P, OUTER // BATCH, TILES, OCTET, SLOTS], FP32)
+        comb_result = keep.tile([P, OUTER // BATCH, TILES, OCTET, SLOTS], FP32)
 
         w_raw, yn_raw, grouped, w_codes, w_scales = {}, {}, {}, {}, {}
         se_rows, norm_factor, se2_rows, slots_bank, se2_grouped = {}, {}, {}, {}, {}
-        yn_bank, all_pairs, turned_logits, total = {}, {}, {}, {}
+        yn_bank, all_pairs, turned_logits = {}, {}, {}
 
         def transpose_two(words, first, tag, bufs):
             bank = psum.tile([P, 2, 2, P], FP32, tag=tag, bufs=bufs)
@@ -101,11 +101,9 @@ def tile_hierarchicalsoftmoe2dblock_pb_kernel(tc, yn, means, w_slot2, out_0, out
                     nc.tensor.transpose(bank[:, a, u, :], words[:, first + a, u, :], ident[:])
             return bank
 
-        mean_rows = means.flatten_outer_dims().rearrange("(a p) d -> p a d", p=P)
+        mean_rows = means.flatten_outer_dims().rearrange("(p a) d -> p a d", p=P)
         mean_words = mean_raw[:].bitcast(FP32).rearrange("p a (w u) -> p a u w", u=2)
-        mean_slots = mean_grouped[:].bitcast(FP32).rearrange(
-            "p k (a b m) u -> p a b k m u", a=MEAN_TILES, m=SEGMENTS
-        )
+        mean_slots = mean_grouped[:].bitcast(FP32).rearrange("p (h l) (b m) u -> p l h b m u", l=2, m=SEGMENTS)
 
         def quantise_means():
             nc.vector.quantize_mx(
@@ -128,8 +126,7 @@ def tile_hierarchicalsoftmoe2dblock_pb_kernel(tc, yn, means, w_slot2, out_0, out
             yn_bank[b] = transpose_two(words, first, "turned", 3)
 
         def copy_yn(b):
-            copy = nc.scalar.copy if b % 2 == 0 else nc.vector.tensor_copy
-            copy(
+            nc.scalar.copy(
                 out=yn_slots[:, 2 * b : 2 * b + 2],
                 in_=yn_bank[b][:].rearrange("p g u (k s) -> p g k s u", k=OUTER),
             )
@@ -153,11 +150,7 @@ def tile_hierarchicalsoftmoe2dblock_pb_kernel(tc, yn, means, w_slot2, out_0, out
             grouped[c] = grouped_pool.tile([P, D, PACK], BF16, name="grouped", align_bytes=64)
             to_words = grouped[c][:].rearrange("p (n i) j -> p n j i", i=4)
             from_rows = w_raw[c].rearrange("p j (n i) -> p n j i", i=4)
-            columns = EARLY_VECTOR_COLUMNS if c < EARLY_STEPS else VECTOR_COLUMNS if c < CHUNKS - LATE_STEPS else D
-            fours = columns // 4
-            nc.vector.tensor_copy(out=to_words[:, :fours], in_=from_rows[:, :fours])
-            if columns < D:
-                nc.scalar.copy(out=to_words[:, fours:], in_=from_rows[:, fours:])
+            nc.vector.tensor_copy(out=to_words, in_=from_rows)
 
         def quantise_chunk(c):
             w_codes[c] = codes_pool.tile([P, D], U32, name="w_codes", align_bytes=64)
@@ -211,7 +204,7 @@ def tile_hierarchicalsoftmoe2dblock_pb_kernel(tc, yn, means, w_slot2, out_0, out
                 se2_grouped[k] = work.tile(
                     [P, GROUPS, INNER, SEGMENTS, PACK], BF16, name="se2_grouped", align_bytes=64
                 )
-            copy = nc.scalar.copy if two < CHUNKS // 2 - VECTOR_GROUPS else nc.vector.tensor_copy
+            copy = nc.scalar.copy if two < CHUNKS // 2 - 1 else nc.vector.tensor_copy
             copy(
                 out=se2_grouped[k][:].bitcast(FP32)[:, :, first : first + 2, :, :],
                 in_=slots_bank[two][:].rearrange("p e u (g m) -> p g e m u", m=SEGMENTS),
@@ -239,89 +232,99 @@ def tile_hierarchicalsoftmoe2dblock_pb_kernel(tc, yn, means, w_slot2, out_0, out
                 )
 
         def copy_quadrants(k):
+            batch, k_in = divmod(k, BATCH)
             for quadrant in range(4):
                 rows = slice(32 * quadrant, 32 * quadrant + 32)
                 nc.scalar.copy(
-                    out=two_groups[rows, k // 2, :, :, k % 2],
+                    out=two_groups[rows, batch, :, :, k_in],
                     in_=all_pairs[k][rows, :, 32 * quadrant : 32 * quadrant + 32].rearrange(
                         "p i (h s) -> p h i s", h=2
                     ),
                 )
 
-        def turn(source, pair):
+        def turn(source, batch, t):
             bank = psum.tile([P, 2 * TURN_STRIDE], FP32, tag="turned", name="bank", bufs=3)
+            columns = source[:, batch].rearrange("p h i k s -> p h (i k s)")
             for h in range(2):
-                nc.tensor.transpose(bank[:, h * P : (h + 1) * P], source[h], ident[:])
+                nc.tensor.transpose(bank[:, h * P : (h + 1) * P], columns[:, h, t * P : (t + 1) * P], ident[:])
             halves = bank[:].rearrange("p (h r) -> p h r", h=2)[:, :, 0:P]
             return halves.rearrange("p h (a b q) -> p a h b q", b=2, q=SLOTS)[:, :, :, 0, :]
 
-        def turn_logits(pair):
-            turned_logits[pair] = turn(
-                [two_groups[:, pair, h].rearrange("p i k s -> p (i k s)") for h in range(2)], pair
-            )
+        def disp_of(values, batch, some):
+            part = values[:, batch, :, :, some]
+            return part.rearrange("p h i k s -> p (h i) k s" if len(part.shape) == 5 else "p h i k -> p (h i) k")
 
-        def find_top(pair, which):
-            if which == COMB:
-                total[pair, COMB] = small.tile([P, OCTET // 2, 2], FP32, name="comb_top")
-                logits = turned_logits[pair]
-            else:
-                total[pair, DISP] = small.tile([P, 2 * OCTETS * 2], FP32, name="disp_top")
-                logits = two_groups[:, pair].rearrange("p h i k s -> p (h i k) s")
-            nc.vector.tensor_reduce(out=total[pair, which][:], in_=logits, axis=AXIS.X, op=ALU.max)
+        def spread(sums):
+            return sums.unsqueeze(len(sums.shape)).to_broadcast(list(sums.shape) + [TOKENS])
 
-        def subtract_top(pair, which):
-            if which == COMB:
-                out = comb_powers[:, pair].rearrange("p (a h) q -> p a h q", h=2)
-                logits = turned_logits[pair]
-                tops = total[pair, COMB][:].unsqueeze(3).to_broadcast([P, OCTET // 2, 2, SLOTS])
-            else:
-                out = disp_powers[:, pair]
-                logits = two_groups[:, pair].rearrange("p h i k s -> p (h i k) s")
-                tops = total[pair, DISP][:].unsqueeze(2).to_broadcast([P, 2 * OCTETS * 2, TOKENS])
-            nc.vector.tensor_tensor(out=out, in0=logits, in1=tops, op=ALU.subtract)
+        def disp_shift(batch, some):
+            logits, tops = disp_of(two_groups, batch, some), disp_of(disp_sums, batch, some)
+            nc.vector.tensor_reduce(out=tops, in_=logits, axis=AXIS.X, op=ALU.max)
+            nc.vector.tensor_tensor(out=disp_of(disp_powers, batch, some), in0=logits, in1=spread(tops), op=ALU.subtract)
 
-        DISP, COMB = 0, 1
-        POWERS = {DISP: disp_powers, COMB: comb_powers}
-        SETS = {DISP: 2 * OCTETS * 2, COMB: OCTET}
+        def disp_power(batch, some):
+            powers = disp_of(disp_powers, batch, some)
+            nc.scalar.activation(out=powers, in_=powers, func=ACT.Exp)
 
-        def exponentiate(pairs, which):
-            nc.scalar.activation(out=POWERS[which][:, pairs], in_=POWERS[which][:, pairs], func=ACT.Exp)
+        def disp_total(batch, some):
+            totals = disp_of(disp_sums, batch, some)
+            nc.vector.tensor_reduce(out=totals, in_=disp_of(disp_powers, batch, some), axis=AXIS.X, op=ALU.add)
+            return lambda: nc.vector.reciprocal(out=totals, in_=totals)
 
-        def find_total(pairs, which):
-            total[pairs.start, which] = small.tile([P, PAIRS, SETS[which]], FP32, name="disp_total" if which == DISP else "comb_total")
+        def disp_divide(batch, some):
+            powers = disp_of(disp_powers, batch, some)
+            nc.vector.tensor_tensor(out=powers, in0=powers, in1=spread(disp_of(disp_sums, batch, some)), op=ALU.mult)
+
+        def disp_turn(batch):
+            for t in range(TILES):
+                nc.scalar.copy(
+                    out=disp_result[:, batch, t].rearrange("p (a h) q -> p a h q", h=2), in_=turn(disp_powers, batch, t)
+                )
+
+        def turn_logits(batch):
+            for t in range(TILES):
+                turned_logits[batch, t] = turn(two_groups, batch, t)
+
+        def comb_shift(batch):
+            for t in range(TILES):
+                nc.vector.tensor_reduce(
+                    out=comb_sums[:, batch, t], in_=turned_logits[batch, t], axis=AXIS.X, op=ALU.max
+                )
+            for t in range(TILES):
+                nc.vector.tensor_tensor(
+                    out=comb_powers[:, batch, t].rearrange("p (a h) q -> p a h q", h=2),
+                    in0=turned_logits[batch, t],
+                    in1=spread(comb_sums[:, batch, t]),
+                    op=ALU.subtract,
+                )
+
+        def comb_power(batch):
+            powers = comb_powers[:, batch].rearrange("p t g q -> p (t g q)")
+            nc.scalar.activation(out=powers, in_=powers, func=ACT.Exp)
+
+        def comb_total(batch):
+            totals = comb_sums[:, batch].rearrange("p t a h -> p (t a h)")
             nc.vector.tensor_reduce(
-                out=total[pairs.start, which][:, pairs], in_=POWERS[which][:, pairs], axis=AXIS.X, op=ALU.add
+                out=totals, in_=comb_powers[:, batch].rearrange("p t g q -> p (t g) q"), axis=AXIS.X, op=ALU.add
             )
+            return lambda: nc.vector.reciprocal(out=totals, in_=totals)
 
-        def invert_total(pairs, which):
-            some = total[pairs.start, which][:, pairs]
-            nc.vector.reciprocal(out=some, in_=some)
-
-        def divide(pairs, which):
-            count = pairs.stop - pairs.start
+        def comb_divide(batch):
             nc.vector.tensor_tensor(
-                out=comb_result[:, pairs] if which == COMB else disp_powers[:, pairs],
-                in0=POWERS[which][:, pairs],
-                in1=total[pairs.start, which][:, pairs].unsqueeze(3).to_broadcast([P, count, SETS[which], 16]),
+                out=comb_result[:, batch].rearrange("p t g q -> p (t g) q"),
+                in0=comb_powers[:, batch].rearrange("p t g q -> p (t g) q"),
+                in1=spread(comb_sums[:, batch].rearrange("p t a h -> p (t a h)")),
                 op=ALU.mult,
             )
 
-        def turn_disp(pairs):
-            for pair in range(pairs.start, pairs.stop):
-                halves = disp_powers[:, pair].rearrange("p (h r) s -> p h (r s)", h=2)
-                nc.scalar.copy(
-                    out=disp_result[:, pair].rearrange("p (a h) q -> p a h q", h=2),
-                    in_=turn([halves[:, h] for h in range(2)], pair),
+        def store(batch, result, out, queue):
+            rows = BATCH * TOKENS
+            for octet in range(OCTETS):
+                t, i = divmod(octet, P // rows)
+                queue.dma_start(
+                    out=out[octet, :, batch * BATCH : (batch + 1) * BATCH].rearrange("g k s q -> (k s) g q"),
+                    in_=result[rows * i : rows * i + rows, batch, t],
                 )
-
-        def store(pairs, which, queue):
-            out, result = (out_1, comb_result) if which == COMB else (out_0, disp_result)
-            for pair in range(pairs.start, pairs.stop):
-                for b in range(OCTETS):
-                    queue.dma_start(
-                        out=out[b, :, 2 * pair : 2 * pair + 2].rearrange("g k s q -> (k s) g q"),
-                        in_=result[32 * b : 32 * b + 32, pair],
-                    )
 
         def rows_step(c):
             return max(c + ROWS_LAG, MEANS_STEP + 1 + c // 2)
@@ -342,17 +345,13 @@ def tile_hierarchicalsoftmoe2dblock_pb_kernel(tc, yn, means, w_slot2, out_0, out
             return group_step(2 * k + 1) + 1
 
         def tokens_step(k):
-            return YN_QUANTISE_STEP + (k // 2 if k < 2 * FIRST_PAIRS else 2 * k - 3 * FIRST_PAIRS)
+            return CHUNKS + QUANTISE_LAG if k >= LATE_TOKENS_FROM else YN_QUANTISE_STEP + k
 
         def logits_step(k):
-            ready = max(slots_step(k), tokens_step(k)) + 1
-            return ready if k == 0 else max(ready, logits_step(k - 1) + 1)
+            return max(slots_step(k), tokens_step(k)) + (LOGITS_LAG if k < OUTER - 2 else LATE_LOGITS_LAG)
 
         def quadrant_step(k):
             return logits_step(k) + 1
-
-        def pair_step(pair):
-            return quadrant_step(2 * pair + 1) + 1
 
         def at(stage, index, count):
             if 0 <= index < count:
@@ -366,51 +365,21 @@ def tile_hierarchicalsoftmoe2dblock_pb_kernel(tc, yn, means, w_slot2, out_0, out
         def turn_means():
             for first in range(0, MEAN_TILES, 2):
                 bank = transpose_two(mean_words, first, "se_rows", 3)
+                l, m = divmod(first, SEGMENTS)
                 nc.scalar.copy(
-                    out=mean_slots[:, first : first + 2],
-                    in_=bank[:].rearrange("p a u (b k m) -> p a b k m u", k=OUTER, m=SEGMENTS),
+                    out=mean_slots[:, l, :, :, m : m + 2, :],
+                    in_=bank[:].rearrange("p a u (b h) -> p h b a u", h=OUTER // 2),
                 )
 
-        def short_stages(step):
-            stages = []
-            for pair in range(PAIRS - 1):
-                since = step - pair_step(pair)
-                if since == 0:
-                    stages += [(find_top, pair, DISP)]
-                elif since == 1:
-                    stages += [(subtract_top, pair, DISP), (find_top, pair, COMB)]
-                elif since == 2:
-                    stages += [(subtract_top, pair, COMB)]
-            if step == first_exponents + 1:
-                stages += [
-                    (find_total, first_pairs, DISP),
-                    (find_total, first_pairs, COMB),
-                    (invert_total, first_pairs, DISP),
-                    (invert_total, first_pairs, COMB),
-                    (divide, first_pairs, DISP),
-                    (divide, first_pairs, COMB),
-                ]
-            return stages
-
-        def run(stages):
-            for stage in stages:
-                stage[0](*stage[1:])
-
-        for c in range(FIRST_LOADS):
-            load_chunks(c, 1)
+        load_chunks(0, 1)
         for half in (slice(0, MEAN_TILES // 2), slice(MEAN_TILES // 2, MEAN_TILES)):
             nc.sync.dma_start(out=mean_raw[:, half, :], in_=mean_rows[:, half, :])
-        for c in range(FIRST_LOADS, SINGLE_LOADS):
+        for c in range(1, SINGLE_LOADS):
             load_chunks(c, 1)
+        turn_means()
 
-        first_pairs = slice(0, FIRST_PAIRS)
-        next_pair = slice(FIRST_PAIRS, FIRST_PAIRS + 1)
-        last_pair = slice(FIRST_PAIRS + 1, PAIRS)
-        last = PAIRS - 1
-        first_exponents = pair_step(FIRST_PAIRS - 1) + 2
-
-        for step in range(quadrant_step(OUTER - 1)):
-            short = short_stages(step)
+        whole, early, late = slice(0, BATCH), slice(0, BATCH - 2), slice(BATCH - 2, BATCH)
+        for step in range(logits_step(OUTER - 1) + 1):
             if (step - YN_LOAD_STEP) % YN_LOAD_EVERY == 0:
                 at(load_yn, (step - YN_LOAD_STEP) // YN_LOAD_EVERY, OCTETS)
             if step % 2 == 0 and SINGLE_LOADS + step < CHUNKS:
@@ -419,58 +388,53 @@ def tile_hierarchicalsoftmoe2dblock_pb_kernel(tc, yn, means, w_slot2, out_0, out
             due(normalise, normalise_step, CHUNKS, step)
             at(regroup, step, CHUNKS)
             due(find_norm_factor, square_step, CHUNKS, step)
-            if step == MEANS_STEP - 1:
-                turn_means()
             if step == MEANS_STEP:
                 quantise_means()
-            run(short[0:1])
             due(multiply_rows, rows_step, CHUNKS, step)
             due(multiply_slots_and_tokens, logits_step, OUTER, step)
             due(group_slots, group_step, CHUNKS // 2, step)
-            at(copy_yn, step - 1 - YN_FIRST_STEP, YN_BANKS)
-            at(transpose_yn, step - YN_FIRST_STEP, YN_BANKS)
+            due(copy_yn, lambda b: YN_FIRST_STEP + b + 1, YN_BANKS, step)
+            due(transpose_yn, lambda b: YN_FIRST_STEP + b, YN_BANKS, step)
             due(turn_slots, turn_step, CHUNKS, step)
-            due(turn_logits, pair_step, PAIRS - 1, step)
             at(quantise_chunk, step - QUANTISE_LAG, CHUNKS)
-            run(short[1:2])
             due(quantise_yn, tokens_step, OUTER, step)
             due(quantise_slots, slots_step, OUTER, step)
-            run(short[2:])
-            due(copy_quadrants, quadrant_step, OUTER, step)
-            if step == first_exponents + 2:
-                turn_disp(first_pairs)
-                for which in (DISP, COMB):
-                    store(first_pairs, which, nc.sync)
-            if step == first_exponents:
-                exponentiate(first_pairs, DISP)
-                exponentiate(first_pairs, COMB)
             if step == normalise_step(CHUNKS - 1) + 1:
-                exponentiate(next_pair, DISP)
-                exponentiate(next_pair, COMB)
+                disp_power(0, whole)
+                comb_power(0)
+            due(copy_quadrants, quadrant_step, OUTER, step)
+            if step == CHUNKS + QUANTISE_LAG - 1 + A_DELAY:
+                turn_logits(0)
+                disp_shift(0, whole)
+                comb_shift(0)
+            if step == CHUNKS + QUANTISE_LAG - 1 + B_DELAY:
+                disp_shift(1, early)
+                disp_power(1, early)
 
-        find_total(next_pair, DISP)
-        find_total(next_pair, COMB)
         copy_quadrants(OUTER - 1)
-        invert_total(next_pair, DISP)
-        invert_total(next_pair, COMB)
-        divide(next_pair, DISP)
-        divide(next_pair, COMB)
-        turn_logits(last)
-        find_top(last, DISP)
-        turn_disp(next_pair)
-        for which in (DISP, COMB):
-            store(next_pair, which, nc.sync)
-        subtract_top(last, DISP)
-        exponentiate(last_pair, DISP)
-        find_top(last, COMB)
-        subtract_top(last, COMB)
-        exponentiate(last_pair, COMB)
-        find_total(last_pair, DISP)
-        invert_total(last_pair, DISP)
-        find_total(last_pair, COMB)
-        divide(last_pair, DISP)
-        turn_disp(last_pair)
-        invert_total(last_pair, COMB)
-        divide(last_pair, COMB)
-        store(last_pair, COMB, nc.sync)
-        store(last_pair, DISP, nc.scalar)
+        invert_disp = disp_total(0, whole)
+        invert_comb = comb_total(0)
+        invert_disp()
+        invert_comb()
+        disp_divide(0, whole)
+        disp_turn(0)
+        store(0, disp_result, out_0, nc.sync)
+        comb_divide(0)
+        store(0, comb_result, out_1, nc.sync)
+        invert_disp = disp_total(1, early)
+        turn_logits(1)
+        disp_shift(1, late)
+        disp_power(1, late)
+        invert_disp()
+        comb_shift(1)
+        comb_power(1)
+        disp_divide(1, early)
+        invert_disp = disp_total(1, late)
+        invert_disp()
+        invert_comb = comb_total(1)
+        disp_divide(1, late)
+        disp_turn(1)
+        invert_comb()
+        comb_divide(1)
+        store(1, comb_result, out_1, nc.sync)
+        store(1, disp_result, out_0, nc.sync)

@@ -35,6 +35,10 @@ PAIR_BUFFERS = 4
 MEANS_STEP = 2
 CODES_BUFFERS = 5
 QUANTISE_LAG = 1
+VECTOR_QUADRANTS = 5
+SHARE_FROM = 2
+SHARE_TO = 5
+SHARED_COLUMNS = 320
 ROWS_LAG = QUANTISE_LAG + 1
 NORMALISE_LAG = 1
 TURN_LAG = 1
@@ -150,7 +154,10 @@ def tile_hierarchicalsoftmoe2dblock_pb_kernel(tc, yn, means, w_slot2, out_0, out
             grouped[c] = grouped_pool.tile([P, D, PACK], BF16, name="grouped", align_bytes=64)
             to_words = grouped[c][:].rearrange("p (n i) j -> p n j i", i=4)
             from_rows = w_raw[c].rearrange("p j (n i) -> p n j i", i=4)
-            nc.vector.tensor_copy(out=to_words, in_=from_rows)
+            fours = (SHARED_COLUMNS if SHARE_FROM <= c < SHARE_TO else D) // 4
+            nc.vector.tensor_copy(out=to_words[:, :fours], in_=from_rows[:, :fours])
+            if fours < D // 4:
+                nc.scalar.copy(out=to_words[:, fours:], in_=from_rows[:, fours:])
 
         def quantise_chunk(c):
             w_codes[c] = codes_pool.tile([P, D], U32, name="w_codes", align_bytes=64)
@@ -235,7 +242,8 @@ def tile_hierarchicalsoftmoe2dblock_pb_kernel(tc, yn, means, w_slot2, out_0, out
             batch, k_in = divmod(k, BATCH)
             for quadrant in range(4):
                 rows = slice(32 * quadrant, 32 * quadrant + 32)
-                nc.scalar.copy(
+                copy = nc.vector.tensor_copy if k == VECTOR_QUADRANTS else nc.scalar.copy
+                copy(
                     out=two_groups[rows, batch, :, :, k_in],
                     in_=all_pairs[k][rows, :, 32 * quadrant : 32 * quadrant + 32].rearrange(
                         "p i (h s) -> p h i s", h=2
@@ -285,11 +293,13 @@ def tile_hierarchicalsoftmoe2dblock_pb_kernel(tc, yn, means, w_slot2, out_0, out
             for t in range(TILES):
                 turned_logits[batch, t] = turn(two_groups, batch, t)
 
-        def comb_shift(batch):
+        def comb_top(batch):
             for t in range(TILES):
                 nc.vector.tensor_reduce(
                     out=comb_sums[:, batch, t], in_=turned_logits[batch, t], axis=AXIS.X, op=ALU.max
                 )
+
+        def comb_shift(batch):
             for t in range(TILES):
                 nc.vector.tensor_tensor(
                     out=comb_powers[:, batch, t].rearrange("p (a h) q -> p a h q", h=2),
@@ -325,6 +335,9 @@ def tile_hierarchicalsoftmoe2dblock_pb_kernel(tc, yn, means, w_slot2, out_0, out
                     out=out[octet, :, batch * BATCH : (batch + 1) * BATCH].rearrange("g k s q -> (k s) g q"),
                     in_=result[rows * i : rows * i + rows, batch, t],
                 )
+
+        def quantise_step(c):
+            return c + QUANTISE_LAG if c > 0 else c
 
         def rows_step(c):
             return max(c + ROWS_LAG, MEANS_STEP + 1 + c // 2)
@@ -388,24 +401,25 @@ def tile_hierarchicalsoftmoe2dblock_pb_kernel(tc, yn, means, w_slot2, out_0, out
             due(normalise, normalise_step, CHUNKS, step)
             at(regroup, step, CHUNKS)
             due(find_norm_factor, square_step, CHUNKS, step)
-            if step == MEANS_STEP:
-                quantise_means()
             due(multiply_rows, rows_step, CHUNKS, step)
             due(multiply_slots_and_tokens, logits_step, OUTER, step)
             due(group_slots, group_step, CHUNKS // 2, step)
             due(copy_yn, lambda b: YN_FIRST_STEP + b + 1, YN_BANKS, step)
             due(transpose_yn, lambda b: YN_FIRST_STEP + b, YN_BANKS, step)
             due(turn_slots, turn_step, CHUNKS, step)
-            at(quantise_chunk, step - QUANTISE_LAG, CHUNKS)
+            due(quantise_chunk, quantise_step, CHUNKS, step)
+            if step == MEANS_STEP:
+                quantise_means()
             due(quantise_yn, tokens_step, OUTER, step)
             due(quantise_slots, slots_step, OUTER, step)
+            due(copy_quadrants, quadrant_step, OUTER, step)
             if step == normalise_step(CHUNKS - 1) + 1:
                 disp_power(0, whole)
                 comb_power(0)
-            due(copy_quadrants, quadrant_step, OUTER, step)
             if step == CHUNKS + QUANTISE_LAG - 1 + A_DELAY:
                 turn_logits(0)
                 disp_shift(0, whole)
+                comb_top(0)
                 comb_shift(0)
             if step == CHUNKS + QUANTISE_LAG - 1 + B_DELAY:
                 disp_shift(1, early)
@@ -417,24 +431,25 @@ def tile_hierarchicalsoftmoe2dblock_pb_kernel(tc, yn, means, w_slot2, out_0, out
         invert_disp()
         invert_comb()
         disp_divide(0, whole)
-        disp_turn(0)
-        store(0, disp_result, out_0, nc.sync)
         comb_divide(0)
         store(0, comb_result, out_1, nc.sync)
         invert_disp = disp_total(1, early)
+        disp_turn(0)
         turn_logits(1)
+        store(0, disp_result, out_0, nc.sync)
         disp_shift(1, late)
         disp_power(1, late)
         invert_disp()
+        disp_divide(1, early)
+        comb_top(1)
+        invert_disp = disp_total(1, late)
         comb_shift(1)
         comb_power(1)
-        disp_divide(1, early)
-        invert_disp = disp_total(1, late)
         invert_disp()
-        invert_comb = comb_total(1)
         disp_divide(1, late)
         disp_turn(1)
+        store(1, disp_result, out_0, nc.sync)
+        invert_comb = comb_total(1)
         invert_comb()
         comb_divide(1)
         store(1, comb_result, out_1, nc.sync)
-        store(1, disp_result, out_0, nc.sync)

@@ -32,29 +32,18 @@ YN_BANKS = GROUPS // 2
 
 SINGLE_LOADS = 4
 PAIR_BUFFERS = 4
-MEANS_STEP = 2
+GROUPED_BUFFERS = 3
 CODES_BUFFERS = 5
-QUANTISE_LAG = 1
-VECTOR_QUADRANTS = 5
-SHARE_FROM = 2
-SHARE_TO = 5
+SHARED_CHUNKS = range(2, 5)
 SHARED_COLUMNS = 320
-ROWS_LAG = QUANTISE_LAG + 1
-NORMALISE_LAG = 1
-TURN_LAG = 1
-GROUP_LAG = 1
+MEANS_STEP = 2
+ROWS_LAG = 2
 YN_LOAD_STEP = 8
 YN_LOAD_EVERY = 4
-LATE_TOKENS_FROM = 6
-A_DELAY = 2
-B_DELAY = 5
-LOGITS_LAG = 1
-LATE_LOGITS_LAG = 3
 YN_FIRST_STEP = 10
 YN_QUANTISE_STEP = YN_FIRST_STEP + YN_BANKS + 1
+LATE_TOKENS = 2
 BATCH = 4
-
-TURN_STRIDE = P + SLOTS
 TILES = OCTETS * BATCH * TOKENS // P
 
 FLOPS = 2 * OUTER * ROWS * D * INNER * D + 2 * GROUPS * OUTER * TOKENS * SLOTS * D
@@ -66,7 +55,7 @@ def tile_hierarchicalsoftmoe2dblock_pb_kernel(tc, yn, means, w_slot2, out_0, out
         ctx.enter_context(tc.manual_schedule())
         keep = ctx.enter_context(tc.tile_pool(name="keep", bufs=1))
         w_pool = ctx.enter_context(tc.tile_pool(name="w_pool", bufs=PAIR_BUFFERS))
-        grouped_pool = ctx.enter_context(tc.tile_pool(name="grouped_pool", bufs=QUANTISE_LAG + 2))
+        grouped_pool = ctx.enter_context(tc.tile_pool(name="grouped_pool", bufs=GROUPED_BUFFERS))
         codes_pool = ctx.enter_context(tc.tile_pool(name="codes_pool", bufs=CODES_BUFFERS))
         work = ctx.enter_context(tc.tile_pool(name="work", bufs=2))
         small = ctx.enter_context(tc.tile_pool(name="small", bufs=6))
@@ -74,6 +63,13 @@ def tile_hierarchicalsoftmoe2dblock_pb_kernel(tc, yn, means, w_slot2, out_0, out
 
         ident = keep.tile([P, P], FP32)
         make_identity(nc, ident[:])
+        parity = keep.tile([P, 2], FP32)
+        nc.vector.tensor_reduce(
+            out=parity[:],
+            in_=ident[:].rearrange("p (q h c) -> p h q c", h=2, c=TOKENS),
+            axis=AXIS.XY,
+            op=ALU.add,
+        )
         warm = keep.tile([P, 1], FP32)
         nc.scalar.activation(out=warm[:], in_=ident[:, 0:1], func=ACT.Abs_reciprocal_sqrt, scale=1.0, bias=1.0)
 
@@ -87,10 +83,11 @@ def tile_hierarchicalsoftmoe2dblock_pb_kernel(tc, yn, means, w_slot2, out_0, out
         se2_codes = keep.tile([P, OUTER, GROUPS * SLOTS], U32, align_bytes=64)
         se2_scales = keep.tile([P, OUTER, GROUPS * SLOTS], U8, align_bytes=64)
         two_groups = keep.tile([P, OUTER // BATCH, 2, OCTETS, BATCH, TOKENS], FP32)
-        disp_powers = keep.tile([P, OUTER // BATCH, 2, OCTETS, BATCH, TOKENS], FP32)
-        disp_sums = keep.tile([P, OUTER // BATCH, 2, OCTETS, BATCH], FP32)
+        logits = keep.tile([P, OUTER // BATCH, OCTETS, BATCH, TOKENS], FP32)
+        disp_powers = keep.tile([P, OUTER // BATCH, OCTETS, BATCH, TOKENS], FP32)
+        disp_sums = keep.tile([P, OUTER // BATCH, OCTETS, BATCH], FP32)
         comb_powers = keep.tile([P, OUTER // BATCH, TILES, OCTET, SLOTS], FP32)
-        comb_sums = keep.tile([P, OUTER // BATCH, TILES, OCTET // 2, 2], FP32)
+        comb_sums = keep.tile([P, OUTER // BATCH, TILES, OCTET], FP32)
         disp_result = keep.tile([P, OUTER // BATCH, TILES, OCTET, SLOTS], FP32)
         comb_result = keep.tile([P, OUTER // BATCH, TILES, OCTET, SLOTS], FP32)
 
@@ -154,10 +151,12 @@ def tile_hierarchicalsoftmoe2dblock_pb_kernel(tc, yn, means, w_slot2, out_0, out
             grouped[c] = grouped_pool.tile([P, D, PACK], BF16, name="grouped", align_bytes=64)
             to_words = grouped[c][:].rearrange("p (n i) j -> p n j i", i=4)
             from_rows = w_raw[c].rearrange("p j (n i) -> p n j i", i=4)
-            fours = (SHARED_COLUMNS if SHARE_FROM <= c < SHARE_TO else D) // 4
-            nc.vector.tensor_copy(out=to_words[:, :fours], in_=from_rows[:, :fours])
-            if fours < D // 4:
+            if c in SHARED_CHUNKS:
+                fours = SHARED_COLUMNS // 4
+                nc.vector.tensor_copy(out=to_words[:, :fours], in_=from_rows[:, :fours])
                 nc.scalar.copy(out=to_words[:, fours:], in_=from_rows[:, fours:])
+            else:
+                nc.vector.tensor_copy(out=to_words, in_=from_rows)
 
         def quantise_chunk(c):
             w_codes[c] = codes_pool.tile([P, D], U32, name="w_codes", align_bytes=64)
@@ -242,7 +241,7 @@ def tile_hierarchicalsoftmoe2dblock_pb_kernel(tc, yn, means, w_slot2, out_0, out
             batch, k_in = divmod(k, BATCH)
             for quadrant in range(4):
                 rows = slice(32 * quadrant, 32 * quadrant + 32)
-                copy = nc.vector.tensor_copy if k == VECTOR_QUADRANTS else nc.scalar.copy
+                copy = nc.vector.tensor_copy if k == OUTER - 3 else nc.scalar.copy
                 copy(
                     out=two_groups[rows, batch, :, :, k_in],
                     in_=all_pairs[k][rows, :, 32 * quadrant : 32 * quadrant + 32].rearrange(
@@ -250,94 +249,107 @@ def tile_hierarchicalsoftmoe2dblock_pb_kernel(tc, yn, means, w_slot2, out_0, out
                     ),
                 )
 
-        def turn(source, batch, t):
-            bank = psum.tile([P, 2 * TURN_STRIDE], FP32, tag="turned", name="bank", bufs=3)
-            columns = source[:, batch].rearrange("p h i k s -> p h (i k s)")
-            for h in range(2):
-                nc.tensor.transpose(bank[:, h * P : (h + 1) * P], columns[:, h, t * P : (t + 1) * P], ident[:])
-            halves = bank[:].rearrange("p (h r) -> p h r", h=2)[:, :, 0:P]
-            return halves.rearrange("p h (a b q) -> p a h b q", b=2, q=SLOTS)[:, :, :, 0, :]
+        def take_even_groups(batch, some):
+            nc.vector.tensor_scalar(
+                out=logits[:, batch, :, some],
+                in0=two_groups[:, batch, 0, :, some],
+                scalar1=parity[:, 0:1],
+                scalar2=None,
+                op0=ALU.mult,
+            )
 
-        def disp_of(values, batch, some):
-            part = values[:, batch, :, :, some]
-            return part.rearrange("p h i k s -> p (h i) k s" if len(part.shape) == 5 else "p h i k -> p (h i) k")
+        def add_odd_groups(batch, some):
+            nc.vector.scalar_tensor_tensor(
+                out=logits[:, batch, :, some],
+                in0=two_groups[:, batch, 1, :, some],
+                scalar=parity[:, 1:2],
+                in1=logits[:, batch, :, some],
+                op0=ALU.mult,
+                op1=ALU.add,
+            )
+
+        def turn(source, batch):
+            bank = psum.tile([P, TILES, OCTET, SLOTS], FP32, tag="turned", name="bank", bufs=3)
+            columns = source[:, batch].rearrange("p i k s -> p (i k s)")
+            for t in range(TILES):
+                nc.tensor.transpose(
+                    bank[:, t].rearrange("p g q -> p (g q)"), columns[:, t * P : (t + 1) * P], ident[:]
+                )
+            return bank[:]
 
         def spread(sums):
-            return sums.unsqueeze(len(sums.shape)).to_broadcast(list(sums.shape) + [TOKENS])
+            return sums.unsqueeze(len(sums.shape)).to_broadcast([P] + list(sums.shape[1:]) + [TOKENS])
+
+        def disp_top(batch, some):
+            nc.vector.tensor_reduce(
+                out=disp_sums[:, batch, :, some], in_=logits[:, batch, :, some], axis=AXIS.X, op=ALU.max
+            )
 
         def disp_shift(batch, some):
-            logits, tops = disp_of(two_groups, batch, some), disp_of(disp_sums, batch, some)
-            nc.vector.tensor_reduce(out=tops, in_=logits, axis=AXIS.X, op=ALU.max)
-            nc.vector.tensor_tensor(out=disp_of(disp_powers, batch, some), in0=logits, in1=spread(tops), op=ALU.subtract)
+            nc.vector.tensor_tensor(
+                out=disp_powers[:, batch, :, some],
+                in0=logits[:, batch, :, some],
+                in1=spread(disp_sums[:, batch, :, some]),
+                op=ALU.subtract,
+            )
 
         def disp_power(batch, some):
-            powers = disp_of(disp_powers, batch, some)
+            powers = disp_powers[:, batch, :, some]
             nc.scalar.activation(out=powers, in_=powers, func=ACT.Exp)
 
         def disp_total(batch, some):
-            totals = disp_of(disp_sums, batch, some)
-            nc.vector.tensor_reduce(out=totals, in_=disp_of(disp_powers, batch, some), axis=AXIS.X, op=ALU.add)
-            return lambda: nc.vector.reciprocal(out=totals, in_=totals)
+            nc.vector.tensor_reduce(
+                out=disp_sums[:, batch, :, some], in_=disp_powers[:, batch, :, some], axis=AXIS.X, op=ALU.add
+            )
+
+        def disp_invert(batch, some):
+            totals = disp_sums[:, batch, :, some]
+            nc.vector.reciprocal(out=totals, in_=totals)
 
         def disp_divide(batch, some):
-            powers = disp_of(disp_powers, batch, some)
-            nc.vector.tensor_tensor(out=powers, in0=powers, in1=spread(disp_of(disp_sums, batch, some)), op=ALU.mult)
+            powers = disp_powers[:, batch, :, some]
+            nc.vector.tensor_tensor(out=powers, in0=powers, in1=spread(disp_sums[:, batch, :, some]), op=ALU.mult)
 
         def disp_turn(batch):
-            for t in range(TILES):
-                nc.scalar.copy(
-                    out=disp_result[:, batch, t].rearrange("p (a h) q -> p a h q", h=2), in_=turn(disp_powers, batch, t)
-                )
+            nc.scalar.copy(out=disp_result[:, batch], in_=turn(disp_powers, batch))
 
         def turn_logits(batch):
-            for t in range(TILES):
-                turned_logits[batch, t] = turn(two_groups, batch, t)
+            turned_logits[batch] = turn(logits, batch)
 
         def comb_top(batch):
-            for t in range(TILES):
-                nc.vector.tensor_reduce(
-                    out=comb_sums[:, batch, t], in_=turned_logits[batch, t], axis=AXIS.X, op=ALU.max
-                )
+            nc.vector.tensor_reduce(out=comb_sums[:, batch], in_=turned_logits[batch], axis=AXIS.X, op=ALU.max)
 
         def comb_shift(batch):
-            for t in range(TILES):
-                nc.vector.tensor_tensor(
-                    out=comb_powers[:, batch, t].rearrange("p (a h) q -> p a h q", h=2),
-                    in0=turned_logits[batch, t],
-                    in1=spread(comb_sums[:, batch, t]),
-                    op=ALU.subtract,
-                )
+            nc.vector.tensor_tensor(
+                out=comb_powers[:, batch], in0=turned_logits[batch], in1=spread(comb_sums[:, batch]), op=ALU.subtract
+            )
 
         def comb_power(batch):
-            powers = comb_powers[:, batch].rearrange("p t g q -> p (t g q)")
+            powers = comb_powers[:, batch]
             nc.scalar.activation(out=powers, in_=powers, func=ACT.Exp)
 
         def comb_total(batch):
-            totals = comb_sums[:, batch].rearrange("p t a h -> p (t a h)")
-            nc.vector.tensor_reduce(
-                out=totals, in_=comb_powers[:, batch].rearrange("p t g q -> p (t g) q"), axis=AXIS.X, op=ALU.add
-            )
-            return lambda: nc.vector.reciprocal(out=totals, in_=totals)
+            nc.vector.tensor_reduce(out=comb_sums[:, batch], in_=comb_powers[:, batch], axis=AXIS.X, op=ALU.add)
+
+        def comb_invert(batch):
+            nc.vector.reciprocal(out=comb_sums[:, batch], in_=comb_sums[:, batch])
 
         def comb_divide(batch):
             nc.vector.tensor_tensor(
-                out=comb_result[:, batch].rearrange("p t g q -> p (t g) q"),
-                in0=comb_powers[:, batch].rearrange("p t g q -> p (t g) q"),
-                in1=spread(comb_sums[:, batch].rearrange("p t a h -> p (t a h)")),
-                op=ALU.mult,
+                out=comb_result[:, batch], in0=comb_powers[:, batch], in1=spread(comb_sums[:, batch]), op=ALU.mult
             )
 
-        def store(batch, result, out, queue):
+        def store(batch, result, out):
             rows = BATCH * TOKENS
             for octet in range(OCTETS):
                 t, i = divmod(octet, P // rows)
-                queue.dma_start(
+                nc.sync.dma_start(
                     out=out[octet, :, batch * BATCH : (batch + 1) * BATCH].rearrange("g k s q -> (k s) g q"),
                     in_=result[rows * i : rows * i + rows, batch, t],
                 )
 
         def quantise_step(c):
-            return c + QUANTISE_LAG if c > 0 else c
+            return c + 1 if c > 0 else c
 
         def rows_step(c):
             return max(c + ROWS_LAG, MEANS_STEP + 1 + c // 2)
@@ -346,110 +358,131 @@ def tile_hierarchicalsoftmoe2dblock_pb_kernel(tc, yn, means, w_slot2, out_0, out
             return rows_step(c) + 1
 
         def normalise_step(c):
-            return square_step(c) + NORMALISE_LAG
+            return square_step(c) + 1
 
         def turn_step(c):
-            return normalise_step(c) + TURN_LAG
+            return normalise_step(c) + 1
 
         def group_step(two):
-            return turn_step(2 * two + 1) + GROUP_LAG
+            return turn_step(2 * two + 1) + 1
 
         def slots_step(k):
             return group_step(2 * k + 1) + 1
 
         def tokens_step(k):
-            return CHUNKS + QUANTISE_LAG if k >= LATE_TOKENS_FROM else YN_QUANTISE_STEP + k
+            return CHUNKS + 1 if k >= OUTER - LATE_TOKENS else YN_QUANTISE_STEP + k
 
         def logits_step(k):
-            return max(slots_step(k), tokens_step(k)) + (LOGITS_LAG if k < OUTER - 2 else LATE_LOGITS_LAG)
+            return max(slots_step(k), tokens_step(k)) + 1
 
         def quadrant_step(k):
             return logits_step(k) + 1
 
-        def at(stage, index, count):
-            if 0 <= index < count:
-                stage(index)
+        def yn_step(b):
+            return YN_FIRST_STEP + b
 
         def due(stage, when, count, step):
             for index in range(count):
                 if when(index) == step:
                     stage(index)
 
-        def turn_means():
-            for first in range(0, MEAN_TILES, 2):
-                bank = transpose_two(mean_words, first, "se_rows", 3)
-                l, m = divmod(first, SEGMENTS)
-                nc.scalar.copy(
-                    out=mean_slots[:, l, :, :, m : m + 2, :],
-                    in_=bank[:].rearrange("p a u (b h) -> p h b a u", h=OUTER // 2),
-                )
-
         load_chunks(0, 1)
         for half in (slice(0, MEAN_TILES // 2), slice(MEAN_TILES // 2, MEAN_TILES)):
             nc.sync.dma_start(out=mean_raw[:, half, :], in_=mean_rows[:, half, :])
         for c in range(1, SINGLE_LOADS):
             load_chunks(c, 1)
-        turn_means()
+        for first in range(0, MEAN_TILES, 2):
+            bank = transpose_two(mean_words, first, "se_rows", 3)
+            l, m = divmod(first, SEGMENTS)
+            nc.scalar.copy(
+                out=mean_slots[:, l, :, :, m : m + 2, :],
+                in_=bank[:].rearrange("p a u (b h) -> p h b a u", h=OUTER // 2),
+            )
 
-        whole, early, late = slice(0, BATCH), slice(0, BATCH - 2), slice(BATCH - 2, BATCH)
-        for step in range(logits_step(OUTER - 1) + 1):
-            if (step - YN_LOAD_STEP) % YN_LOAD_EVERY == 0:
-                at(load_yn, (step - YN_LOAD_STEP) // YN_LOAD_EVERY, OCTETS)
+        last = CHUNKS - 1
+        for step in range(rows_step(last) + 1):
+            for i in range(OCTETS):
+                if step == YN_LOAD_STEP + i * YN_LOAD_EVERY:
+                    load_yn(i)
             if step % 2 == 0 and SINGLE_LOADS + step < CHUNKS:
                 load_chunks(SINGLE_LOADS + step, 2)
             due(square_rows, square_step, CHUNKS, step)
             due(normalise, normalise_step, CHUNKS, step)
-            at(regroup, step, CHUNKS)
+            if step < CHUNKS:
+                regroup(step)
             due(find_norm_factor, square_step, CHUNKS, step)
             due(multiply_rows, rows_step, CHUNKS, step)
             due(multiply_slots_and_tokens, logits_step, OUTER, step)
             due(group_slots, group_step, CHUNKS // 2, step)
-            due(copy_yn, lambda b: YN_FIRST_STEP + b + 1, YN_BANKS, step)
-            due(transpose_yn, lambda b: YN_FIRST_STEP + b, YN_BANKS, step)
+            due(copy_yn, lambda b: yn_step(b) + 1, YN_BANKS, step)
+            due(transpose_yn, yn_step, YN_BANKS, step)
             due(turn_slots, turn_step, CHUNKS, step)
             due(quantise_chunk, quantise_step, CHUNKS, step)
             if step == MEANS_STEP:
                 quantise_means()
             due(quantise_yn, tokens_step, OUTER, step)
             due(quantise_slots, slots_step, OUTER, step)
-            due(copy_quadrants, quadrant_step, OUTER, step)
-            if step == normalise_step(CHUNKS - 1) + 1:
-                disp_power(0, whole)
-                comb_power(0)
-            if step == CHUNKS + QUANTISE_LAG - 1 + A_DELAY:
-                turn_logits(0)
-                disp_shift(0, whole)
-                comb_top(0)
-                comb_shift(0)
-            if step == CHUNKS + QUANTISE_LAG - 1 + B_DELAY:
-                disp_shift(1, early)
-                disp_power(1, early)
+            due(copy_quadrants, quadrant_step, BATCH, step)
 
+        whole, early, late = slice(0, BATCH), slice(0, BATCH - 2), slice(BATCH - 2, BATCH)
+        square_rows(last)
+        normalise(last - 1)
+        find_norm_factor(last)
+        turn_slots(last - 2)
+        take_even_groups(0, whole)
+        quantise_slots(OUTER - 2)
+        add_odd_groups(0, whole)
+        copy_quadrants(OUTER - 3)
+        turn_slots(last - 1)
+        turn_logits(0)
+        normalise(last)
+        copy_quadrants(OUTER - 4)
+        group_slots(CHUNKS // 2 - 2)
+        disp_top(0, whole)
+        turn_slots(last)
+        comb_top(0)
+        disp_shift(0, whole)
+        comb_shift(0)
+        disp_power(0, whole)
+        comb_power(0)
+        group_slots(CHUNKS // 2 - 1)
+        take_even_groups(1, early)
+        quantise_slots(OUTER - 1)
+        multiply_slots_and_tokens(OUTER - 2)
+        copy_quadrants(OUTER - 2)
+        multiply_slots_and_tokens(OUTER - 1)
+        add_odd_groups(1, early)
+        disp_total(0, whole)
+        disp_top(1, early)
+        comb_total(0)
         copy_quadrants(OUTER - 1)
-        invert_disp = disp_total(0, whole)
-        invert_comb = comb_total(0)
-        invert_disp()
-        invert_comb()
+        disp_shift(1, early)
+        disp_power(1, early)
+        disp_invert(0, whole)
+        comb_invert(0)
         disp_divide(0, whole)
+        take_even_groups(1, late)
         comb_divide(0)
-        store(0, comb_result, out_1, nc.sync)
-        invert_disp = disp_total(1, early)
+        store(0, comb_result, out_1)
+        add_odd_groups(1, late)
         disp_turn(0)
+        store(0, disp_result, out_0)
         turn_logits(1)
-        store(0, disp_result, out_0, nc.sync)
+        disp_total(1, early)
+        disp_top(1, late)
+        disp_invert(1, early)
         disp_shift(1, late)
         disp_power(1, late)
-        invert_disp()
-        disp_divide(1, early)
         comb_top(1)
-        invert_disp = disp_total(1, late)
+        disp_divide(1, early)
         comb_shift(1)
         comb_power(1)
-        invert_disp()
+        disp_total(1, late)
+        disp_invert(1, late)
+        comb_total(1)
         disp_divide(1, late)
         disp_turn(1)
-        store(1, disp_result, out_0, nc.sync)
-        invert_comb = comb_total(1)
-        invert_comb()
+        store(1, disp_result, out_0)
+        comb_invert(1)
         comb_divide(1)
-        store(1, comb_result, out_1, nc.sync)
+        store(1, comb_result, out_1)

@@ -482,7 +482,7 @@ def tile_hierarchicalsoftmoe2dblock_pb_kernel(tc, yn, means, w_slot2, out_0, out
         comb_total(1)
         disp_divide(1, late)
         disp_turn(1)
-        store(1, disp_result, out_0)
         comb_invert(1)
         comb_divide(1)
         store(1, comb_result, out_1)
+        store(1, disp_result, out_0)

from contextlib import ExitStack

import concourse.mybir as mybir
from concourse.masks import make_identity

FP32 = mybir.dt.float32
BF16 = mybir.dt.bfloat16
U32 = mybir.dt.uint32
U8 = mybir.dt.uint8
FP8X4 = mybir.dt.float8_e4m3fn_x4
ALU = mybir.AluOpType
ACT = mybir.ActivationFunctionType
AXIS = mybir.AxisListType

P = 128
PACK = 4
GROUPS = 32
OUTER = 8
TOKENS = 16
INNER = 4
SEGMENTS = 4
SLOTS = INNER * SEGMENTS
D = 512
ROWS = GROUPS * SEGMENTS
OCTET = P // TOKENS
OCTETS = GROUPS // OCTET
EPS = 1e-6

CHUNKS = OUTER * INNER
MEAN_TILES = GROUPS * OUTER * SEGMENTS // P
YN_BANKS = GROUPS // 2

SINGLE_LOADS = 4
PAIR_BUFFERS = 4
GROUPED_BUFFERS = 3
CODES_BUFFERS = 5
SHARED_CHUNKS = range(2, 5)
SHARED_COLUMNS = 320
MEANS_STEP = 2
ROWS_LAG = 2
YN_LOAD_STEP = 8
YN_LOAD_EVERY = 4
YN_FIRST_STEP = 10
YN_QUANTISE_STEP = YN_FIRST_STEP + YN_BANKS + 1
LATE_TOKENS = 2
BATCH = 4
TILES = OCTETS * BATCH * TOKENS // P

FLOPS = 2 * OUTER * ROWS * D * INNER * D + 2 * GROUPS * OUTER * TOKENS * SLOTS * D


def tile_hierarchicalsoftmoe2dblock_pb_kernel(tc, yn, means, w_slot2, out_0, out_1):
    nc = tc.nc
    with ExitStack() as ctx:
        ctx.enter_context(tc.manual_schedule())
        keep = ctx.enter_context(tc.tile_pool(name="keep", bufs=1))
        w_pool = ctx.enter_context(tc.tile_pool(name="w_pool", bufs=PAIR_BUFFERS))
        grouped_pool = ctx.enter_context(tc.tile_pool(name="grouped_pool", bufs=GROUPED_BUFFERS))
        codes_pool = ctx.enter_context(tc.tile_pool(name="codes_pool", bufs=CODES_BUFFERS))
        work = ctx.enter_context(tc.tile_pool(name="work", bufs=2))
        small = ctx.enter_context(tc.tile_pool(name="small", bufs=6))
        psum = ctx.enter_context(tc.psum_pool(name="psum", bufs=2))

        ident = keep.tile([P, P], FP32)
        make_identity(nc, ident[:])
        parity = keep.tile([P, 2], FP32)
        nc.vector.tensor_reduce(
            out=parity[:],
            in_=ident[:].rearrange("p (q h c) -> p h q c", h=2, c=TOKENS),
            axis=AXIS.XY,
            op=ALU.add,
        )
        warm = keep.tile([P, 1], FP32)
        nc.scalar.activation(out=warm[:], in_=ident[:, 0:1], func=ACT.Abs_reciprocal_sqrt, scale=1.0, bias=1.0)

        mean_raw = keep.tile([P, MEAN_TILES, D], BF16)
        mean_grouped = keep.tile([P, OUTER, ROWS, PACK], BF16, align_bytes=64)
        mean_codes = keep.tile([P, OUTER, ROWS], U32, align_bytes=64)
        mean_scales = keep.tile([P, OUTER, ROWS], U8, align_bytes=64)
        yn_grouped = keep.tile([P, OUTER, GROUPS, TOKENS, PACK], BF16, align_bytes=64)
        yn_codes = keep.tile([P, OUTER, GROUPS * TOKENS], U32, align_bytes=64)
        yn_scales = keep.tile([P, OUTER, GROUPS * TOKENS], U8, align_bytes=64)
        se2_codes = keep.tile([P, OUTER, GROUPS * SLOTS], U32, align_bytes=64)
        se2_scales = keep.tile([P, OUTER, GROUPS * SLOTS], U8, align_bytes=64)
        two_groups = keep.tile([P, OUTER // BATCH, 2, OCTETS, BATCH, TOKENS], FP32)
        logits = keep.tile([P, OUTER // BATCH, OCTETS, BATCH, TOKENS], FP32)
        disp_powers = keep.tile([P, OUTER // BATCH, OCTETS, BATCH, TOKENS], FP32)
        disp_sums = keep.tile([P, OUTER // BATCH, OCTETS, BATCH], FP32)
        comb_powers = keep.tile([P, OUTER // BATCH, TILES, OCTET, SLOTS], FP32)
        comb_sums = keep.tile([P, OUTER // BATCH, TILES, OCTET], FP32)
        disp_result = keep.tile([P, OUTER // BATCH, TILES, OCTET, SLOTS], FP32)
        comb_result = keep.tile([P, OUTER // BATCH, TILES, OCTET, SLOTS], FP32)

        w_raw, yn_raw, grouped, w_codes, w_scales = {}, {}, {}, {}, {}
        se_rows, norm_factor, se2_rows, slots_bank, se2_grouped = {}, {}, {}, {}, {}
        yn_bank, all_pairs, turned_logits = {}, {}, {}

        def transpose_two(words, first, tag, bufs):
            bank = psum.tile([P, 2, 2, P], FP32, tag=tag, bufs=bufs)
            for a in range(2):
                for u in range(2):
                    nc.tensor.transpose(bank[:, a, u, :], words[:, first + a, u, :], ident[:])
            return bank

        mean_rows = means.flatten_outer_dims().rearrange("(p a) d -> p a d", p=P)
        mean_words = mean_raw[:].bitcast(FP32).rearrange("p a (w u) -> p a u w", u=2)
        mean_slots = mean_grouped[:].bitcast(FP32).rearrange("p (h l) (b m) u -> p l h b m u", l=2, m=SEGMENTS)

        def quantise_means():
            nc.vector.quantize_mx(
                out=mean_codes[:].rearrange("p k r -> p (k r)").bitcast(FP8X4),
                scales=mean_scales[:].rearrange("p k r -> p (k r)"),
                in_=mean_grouped[:].rearrange("p k r t -> p (k r t)"),
            )

        yn_rows = yn.flatten_outer_dims().rearrange("(g p) d -> p g d", p=P)
        yn_slots = yn_grouped[:].bitcast(FP32).rearrange("p k g s u -> p g k s u")

        def load_yn(i):
            some = slice(i * OCTET, (i + 1) * OCTET)
            yn_raw[i] = w_pool.tile([P, OCTET, D], BF16, name="yn_raw", bufs=2)
            nc.sync.dma_start(out=yn_raw[i][:], in_=yn_rows[:, some, :])

        def transpose_yn(b):
            i, first = divmod(2 * b, OCTET)
            words = yn_raw[i][:].bitcast(FP32).rearrange("p g (u w) -> p g u w", u=2)
            yn_bank[b] = transpose_two(words, first, "turned", 3)

        def copy_yn(b):
            nc.scalar.copy(
                out=yn_slots[:, 2 * b : 2 * b + 2],
                in_=yn_bank[b][:].rearrange("p g u (k s) -> p g k s u", k=OUTER),
            )

        def quantise_yn(k):
            nc.vector.quantize_mx(
                out=yn_codes[:, k, :].bitcast(FP8X4),
                scales=yn_scales[:, k, :],
                in_=yn_grouped[:, k].rearrange("p g s t -> p (g s t)"),
            )

        def load_chunks(c, count):
            k, e = divmod(c, INNER)
            both = w_pool.tile([P, PACK, count * D], BF16, name="w_single" if count == 1 else "w_pair")
            rows = w_slot2[k].rearrange("(p j) n -> p j n", j=PACK)
            nc.sync.dma_start(out=both[:], in_=rows[:, :, e * D : (e + count) * D])
            for i in range(count):
                w_raw[c + i] = both[:, :, i * D : (i + 1) * D]

        def regroup(c):
            grouped[c] = grouped_pool.tile([P, D, PACK], BF16, name="grouped", align_bytes=64)
            to_words = grouped[c][:].rearrange("p (n i) j -> p n j i", i=4)
            from_rows = w_raw[c].rearrange("p j (n i) -> p n j i", i=4)
            if c in SHARED_CHUNKS:
                fours = SHARED_COLUMNS // 4
                nc.vector.tensor_copy(out=to_words[:, :fours], in_=from_rows[:, :fours])
                nc.scalar.copy(out=to_words[:, fours:], in_=from_rows[:, fours:])
            else:
                nc.vector.tensor_copy(out=to_words, in_=from_rows)

        def quantise_chunk(c):
            w_codes[c] = codes_pool.tile([P, D], U32, name="w_codes", align_bytes=64)
            w_scales[c] = codes_pool.tile([P, D], U8, name="w_scales", align_bytes=64)
            nc.vector.quantize_mx(
                out=w_codes[c][:].bitcast(FP8X4),
                scales=w_scales[c][:],
                in_=grouped[c][:].rearrange("p n j -> p (n j)"),
            )

        def multiply_rows(c):
            se_rows[c] = psum.tile([P, D], FP32, name="se_rows", bufs=3)
            nc.tensor.matmul_mx(
                out=se_rows[c][:],
                lhsT=mean_codes[:, c // INNER, :].bitcast(FP8X4),
                lhsT_scale=mean_scales[:, c // INNER, :],
                rhs=w_codes[c][:].bitcast(FP8X4),
                rhs_scale=w_scales[c][:],
                start=True,
                stop=True,
            )

        def square_rows(c):
            norm_factor[c] = small.tile([P, 1], FP32, name="norm_factor")
            squares = work.tile([P, D], BF16)
            nc.scalar.activation(out=squares[:], in_=se_rows[c][:], func=ACT.Square, accum_out=norm_factor[c][:])

        def find_norm_factor(c):
            nc.scalar.activation(
                out=norm_factor[c][:],
                in_=norm_factor[c][:],
                func=ACT.Abs_reciprocal_sqrt,
                scale=1.0 / D,
                bias=EPS / D,
            )

        def normalise(c):
            se2_rows[c] = work.tile([P, D], BF16, name="se2_rows", bufs=3)
            nc.scalar.activation(out=se2_rows[c][:], in_=se_rows[c][:], func=ACT.Copy, scale=norm_factor[c][:])

        def turn_slots(c):
            if c % 2 == 0:
                slots_bank[c // 2] = psum.tile([P, 2, 2, P], FP32, name="slots_bank")
            words = se2_rows[c][:].bitcast(FP32).rearrange("p (u w) -> p u w", u=2)
            for u in range(2):
                nc.tensor.transpose(slots_bank[c // 2][:, c % 2, u, :], words[:, u, :], ident[:])

        def group_slots(two):
            k, first = divmod(2 * two, INNER)
            if first == 0:
                se2_grouped[k] = work.tile(
                    [P, GROUPS, INNER, SEGMENTS, PACK], BF16, name="se2_grouped", align_bytes=64
                )
            copy = nc.scalar.copy if two < CHUNKS // 2 - 1 else nc.vector.tensor_copy
            copy(
                out=se2_grouped[k][:].bitcast(FP32)[:, :, first : first + 2, :, :],
                in_=slots_bank[two][:].rearrange("p e u (g m) -> p g e m u", m=SEGMENTS),
            )

        def quantise_slots(k):
            nc.vector.quantize_mx(
                out=se2_codes[:, k, :].bitcast(FP8X4),
                scales=se2_scales[:, k, :],
                in_=se2_grouped[k][:].rearrange("p g e m t -> p (g e m t)"),
            )

        def multiply_slots_and_tokens(k):
            all_pairs[k] = psum.tile([P, OCTETS, P], FP32, tag="turned", name="all_pairs", bufs=3)
            for i in range(OCTETS):
                block = slice(i * P, (i + 1) * P)
                nc.tensor.matmul_mx(
                    out=all_pairs[k][:, i, :],
                    lhsT=se2_codes[:, k, block].bitcast(FP8X4),
                    lhsT_scale=se2_scales[:, k, block],
                    rhs=yn_codes[:, k, block].bitcast(FP8X4),
                    rhs_scale=yn_scales[:, k, block],
                    start=True,
                    stop=True,
                )

        def copy_quadrants(k):
            batch, k_in = divmod(k, BATCH)
            for quadrant in range(4):
                rows = slice(32 * quadrant, 32 * quadrant + 32)
                copy = nc.vector.tensor_copy if k == OUTER - 3 else nc.scalar.copy
                copy(
                    out=two_groups[rows, batch, :, :, k_in],
                    in_=all_pairs[k][rows, :, 32 * quadrant : 32 * quadrant + 32].rearrange(
                        "p i (h s) -> p h i s", h=2
                    ),
                )

        def take_even_groups(batch, some):
            nc.vector.tensor_scalar(
                out=logits[:, batch, :, some],
                in0=two_groups[:, batch, 0, :, some],
                scalar1=parity[:, 0:1],
                scalar2=None,
                op0=ALU.mult,
            )

        def add_odd_groups(batch, some):
            nc.vector.scalar_tensor_tensor(
                out=logits[:, batch, :, some],
                in0=two_groups[:, batch, 1, :, some],
                scalar=parity[:, 1:2],
                in1=logits[:, batch, :, some],
                op0=ALU.mult,
                op1=ALU.add,
            )

        def turn(source, batch):
            bank = psum.tile([P, TILES, OCTET, SLOTS], FP32, tag="turned", name="bank", bufs=3)
            columns = source[:, batch].rearrange("p i k s -> p (i k s)")
            for t in range(TILES):
                nc.tensor.transpose(
                    bank[:, t].rearrange("p g q -> p (g q)"), columns[:, t * P : (t + 1) * P], ident[:]
                )
            return bank[:]

        def spread(sums):
            return sums.unsqueeze(len(sums.shape)).to_broadcast([P] + list(sums.shape[1:]) + [TOKENS])

        def disp_top(batch, some):
            nc.vector.tensor_reduce(
                out=disp_sums[:, batch, :, some], in_=logits[:, batch, :, some], axis=AXIS.X, op=ALU.max
            )

        def disp_shift(batch, some):
            nc.vector.tensor_tensor(
                out=disp_powers[:, batch, :, some],
                in0=logits[:, batch, :, some],
                in1=spread(disp_sums[:, batch, :, some]),
                op=ALU.subtract,
            )

        def disp_power(batch, some):
            powers = disp_powers[:, batch, :, some]
            nc.scalar.activation(out=powers, in_=powers, func=ACT.Exp)

        def disp_total(batch, some):
            nc.vector.tensor_reduce(
                out=disp_sums[:, batch, :, some], in_=disp_powers[:, batch, :, some], axis=AXIS.X, op=ALU.add
            )

        def disp_invert(batch, some):
            totals = disp_sums[:, batch, :, some]
            nc.vector.reciprocal(out=totals, in_=totals)

        def disp_divide(batch, some):
            powers = disp_powers[:, batch, :, some]
            nc.vector.tensor_tensor(out=powers, in0=powers, in1=spread(disp_sums[:, batch, :, some]), op=ALU.mult)

        def disp_turn(batch):
            nc.scalar.copy(out=disp_result[:, batch], in_=turn(disp_powers, batch))

        def turn_logits(batch):
            turned_logits[batch] = turn(logits, batch)

        def comb_top(batch):
            nc.vector.tensor_reduce(out=comb_sums[:, batch], in_=turned_logits[batch], axis=AXIS.X, op=ALU.max)

        def comb_shift(batch):
            nc.vector.tensor_tensor(
                out=comb_powers[:, batch], in0=turned_logits[batch], in1=spread(comb_sums[:, batch]), op=ALU.subtract
            )

        def comb_power(batch):
            powers = comb_powers[:, batch]
            nc.scalar.activation(out=powers, in_=powers, func=ACT.Exp)

        def comb_total(batch):
            nc.vector.tensor_reduce(out=comb_sums[:, batch], in_=comb_powers[:, batch], axis=AXIS.X, op=ALU.add)

        def comb_invert(batch):
            nc.vector.reciprocal(out=comb_sums[:, batch], in_=comb_sums[:, batch])

        def comb_divide(batch):
            nc.vector.tensor_tensor(
                out=comb_result[:, batch], in0=comb_powers[:, batch], in1=spread(comb_sums[:, batch]), op=ALU.mult
            )

        def store(batch, result, out):
            rows = BATCH * TOKENS
            for octet in range(OCTETS):
                t, i = divmod(octet, P // rows)
                nc.sync.dma_start(
                    out=out[octet, :, batch * BATCH : (batch + 1) * BATCH].rearrange("g k s q -> (k s) g q"),
                    in_=result[rows * i : rows * i + rows, batch, t],
                )

        def quantise_step(c):
            return c + 1 if c > 0 else c

        def rows_step(c):
            return max(c + ROWS_LAG, MEANS_STEP + 1 + c // 2)

        def square_step(c):
            return rows_step(c) + 1

        def normalise_step(c):
            return square_step(c) + 1

        def turn_step(c):
            return normalise_step(c) + 1

        def group_step(two):
            return turn_step(2 * two + 1) + 1

        def slots_step(k):
            return group_step(2 * k + 1) + 1

        def tokens_step(k):
            return CHUNKS + 1 if k >= OUTER - LATE_TOKENS else YN_QUANTISE_STEP + k

        def logits_step(k):
            return max(slots_step(k), tokens_step(k)) + 1

        def quadrant_step(k):
            return logits_step(k) + 1

        def yn_step(b):
            return YN_FIRST_STEP + b

        def due(stage, when, count, step):
            for index in range(count):
                if when(index) == step:
                    stage(index)

        load_chunks(0, 1)
        for half in (slice(0, MEAN_TILES // 2), slice(MEAN_TILES // 2, MEAN_TILES)):
            nc.sync.dma_start(out=mean_raw[:, half, :], in_=mean_rows[:, half, :])
        for c in range(1, SINGLE_LOADS):
            load_chunks(c, 1)
        for first in range(0, MEAN_TILES, 2):
            bank = transpose_two(mean_words, first, "se_rows", 3)
            l, m = divmod(first, SEGMENTS)
            nc.scalar.copy(
                out=mean_slots[:, l, :, :, m : m + 2, :],
                in_=bank[:].rearrange("p a u (b h) -> p h b a u", h=OUTER // 2),
            )

        last = CHUNKS - 1
        for step in range(rows_step(last) + 1):
            for i in range(OCTETS):
                if step == YN_LOAD_STEP + i * YN_LOAD_EVERY:
                    load_yn(i)
            if step % 2 == 0 and SINGLE_LOADS + step < CHUNKS:
                load_chunks(SINGLE_LOADS + step, 2)
            due(square_rows, square_step, CHUNKS, step)
            due(normalise, normalise_step, CHUNKS, step)
            if step < CHUNKS:
                regroup(step)
            due(find_norm_factor, square_step, CHUNKS, step)
            due(multiply_rows, rows_step, CHUNKS, step)
            due(multiply_slots_and_tokens, logits_step, OUTER, step)
            due(group_slots, group_step, CHUNKS // 2, step)
            due(copy_yn, lambda b: yn_step(b) + 1, YN_BANKS, step)
            due(transpose_yn, yn_step, YN_BANKS, step)
            due(turn_slots, turn_step, CHUNKS, step)
            due(quantise_chunk, quantise_step, CHUNKS, step)
            if step == MEANS_STEP:
                quantise_means()
            due(quantise_yn, tokens_step, OUTER, step)
            due(quantise_slots, slots_step, OUTER, step)
            due(copy_quadrants, quadrant_step, BATCH, step)

        whole, early, late = slice(0, BATCH), slice(0, BATCH - 2), slice(BATCH - 2, BATCH)
        square_rows(last)
        normalise(last - 1)
        find_norm_factor(last)
        turn_slots(last - 2)
        take_even_groups(0, whole)
        quantise_slots(OUTER - 2)
        add_odd_groups(0, whole)
        copy_quadrants(OUTER - 3)
        turn_slots(last - 1)
        turn_logits(0)
        normalise(last)
        copy_quadrants(OUTER - 4)
        group_slots(CHUNKS // 2 - 2)
        disp_top(0, whole)
        turn_slots(last)
        comb_top(0)
        disp_shift(0, whole)
        comb_shift(0)
        disp_power(0, whole)
        comb_power(0)
        group_slots(CHUNKS // 2 - 1)
        take_even_groups(1, early)
        quantise_slots(OUTER - 1)
        multiply_slots_and_tokens(OUTER - 2)
        copy_quadrants(OUTER - 2)
        multiply_slots_and_tokens(OUTER - 1)
        add_odd_groups(1, early)
        disp_total(0, whole)
        disp_top(1, early)
        comb_total(0)
        copy_quadrants(OUTER - 1)
        disp_shift(1, early)
        disp_power(1, early)
        disp_invert(0, whole)
        comb_invert(0)
        disp_divide(0, whole)
        take_even_groups(1, late)
        comb_divide(0)
        store(0, comb_result, out_1)
        add_odd_groups(1, late)
        disp_turn(0)
        store(0, disp_result, out_0)
        turn_logits(1)
        disp_total(1, early)
        disp_top(1, late)
        disp_invert(1, early)
        disp_shift(1, late)
        disp_power(1, late)
        comb_top(1)
        disp_divide(1, early)
        comb_shift(1)
        comb_power(1)
        disp_total(1, late)
        disp_invert(1, late)
        comb_total(1)
        disp_divide(1, late)
        disp_turn(1)
        comb_invert(1)
        comb_divide(1)
        store(1, comb_result, out_1)
        store(1, disp_result, out_0)
